import numpy as np
import ml_dtypes


def mxq(x, axis, fmt="e4m3"):
    dtype, down = {"e4m3": (ml_dtypes.float8_e4m3fn, 7), "e5m2": (ml_dtypes.float8_e5m2, 14)}[fmt]
    v = np.moveaxis(np.asarray(x, np.float32).astype(ml_dtypes.bfloat16).astype(np.float64), axis, -1)
    blocks = v.reshape(v.shape[:-1] + (-1, 32))
    amax = np.abs(blocks).max(-1, keepdims=True)
    byte = np.maximum(np.where(amax > 0, np.frexp(amax)[1] - 1 + 127, 0) - down, 1)
    scale = np.exp2(byte - 127.0)
    codes = (blocks / scale).astype(np.float32).astype(dtype).astype(np.float64)
    return np.moveaxis((codes * scale).reshape(v.shape), -1, axis)


WIDE = False


def mx_kscale(k):
    if not WIDE:
        return np.ones(k)
    levels = np.array([10, -10, 5, -5, 0])
    a = np.random.permutation(np.resize(levels, k // 512 * 4)).reshape(k // 512, 4)
    idx = np.arange(k)
    return np.exp2(a[idx // 512, idx % 128 // 32])


BF16 = ml_dtypes.bfloat16


def bf(x):
    return np.asarray(x, np.float32).astype(BF16)


def f64(x):
    return np.asarray(x).astype(np.float64)


E2M1 = np.array([0.0, 0.5, 1.0, 1.5, 2.0, 3.0, 4.0, 6.0, -0.0, -0.5, -1.0, -1.5, -2.0, -3.0, -4.0, -6.0])


def pack_weight(w, fmt):
    k, n = w.shape
    w = f64(bf(w)).reshape(k // 32, 32, n)
    amax = np.abs(w).max(1)
    if fmt == "e4m3":
        byte = np.frexp(amax)[1] - 1 + 127 - 7
    else:
        mant, ex = np.frexp(amax / 6.0)
        byte = np.where(mant > 0.5, ex, ex - 1) + 127
    byte = np.clip(np.where(amax > 0, byte, 1), 1, 254)
    scaled = (w * np.exp2(127.0 - byte)[:, None, :]).reshape(k, n).astype(np.float32)
    by_word = np.ascontiguousarray(scaled.reshape(k // 512, 128, 4, n).transpose(0, 1, 3, 2))
    if fmt == "e4m3":
        words = by_word.astype(ml_dtypes.float8_e4m3fn).view(np.uint8)
    else:
        c = by_word.astype(ml_dtypes.float4_e2m1fn).view(np.uint8) & 0xF
        words = c[..., 0::2] | (c[..., 1::2] << 4)
    return np.ascontiguousarray(words), np.ascontiguousarray(byte.astype(np.uint8).reshape(k // 512, 16, n))


def unpack_weight(words, scales, fmt):
    g, p, n, _ = words.shape
    if fmt == "e4m3":
        vals = np.ascontiguousarray(words).view(ml_dtypes.float8_e4m3fn).astype(np.float64)
    else:
        nib = np.empty((g, p, n, 4), np.uint8)
        nib[..., 0::2] = words & 0xF
        nib[..., 1::2] = words >> 4
        vals = E2M1[nib]
    vals = vals * np.repeat(np.exp2(scales.astype(np.float64) - 127.0), 8, axis=1)[..., None]
    return vals.transpose(0, 1, 3, 2).reshape(g * 512, n)


B, Q, K, D = 8, 1024, 512, 512
NEG = -10000.0
FMT = "e4m3"


def setup_inputs():
    s, t = mx_kscale(D), mx_kscale(D)
    query = bf(np.random.standard_normal((B, Q, D)) * s)
    context = bf(np.random.standard_normal((B, K, D)) * 0.5 / t)
    query_bit = bf(np.random.random((B, Q)) > 0.25)
    context_bit = bf(np.random.random((B, K)) > 0.25)
    w = np.random.standard_normal((D, D)) * 4.0 / D * t[:, None] / s[None, :]
    words, scales = pack_weight(np.ascontiguousarray(w.T), FMT)
    b_in = bf(np.random.standard_normal(D) / np.sqrt(D) * t)
    return {"query": query,
            "context": context,
            "query_bit": query_bit,
            "context_bit": context_bit,
            "W_in_words": words,
            "W_in_scales": scales,
            "b_in": b_in}


def reference(query, context, query_bit, context_bit, W_in_words, W_in_scales, b_in):
    ext = (1.0 - f64(query_bit)[:, :, None] * f64(context_bit)[:, None, :]) * NEG
    q = (mxq(f64(query), 2, "e4m3") @ unpack_weight(W_in_words, W_in_scales, FMT)) + f64(b_in)
    scores = (mxq(q, 2, "e4m3") @ mxq(f64(context), 2, "e4m3").transpose(0, 2, 1)) + ext
    e = np.exp(scores - scores.max(-1, keepdims=True))
    return e / e.sum(-1, keepdims=True)

@@ -1,0 +1,325 @@
+from contextlib import ExitStack
+
+import concourse.mybir as mybir
+from concourse.masks import make_identity
+
+F32 = mybir.dt.float32
+BF16 = mybir.dt.bfloat16
+I32 = mybir.dt.int32
+U32 = mybir.dt.uint32
+U8 = mybir.dt.uint8
+FP8X4 = mybir.dt.float8_e4m3fn_x4
+ALU = mybir.AluOpType
+ACT = mybir.ActivationFunctionType
+AXIS = mybir.AxisListType
+
+P = 128
+PACK = 4
+BATCHES, Q_ROWS, C_ROWS, FEATURES = 8, 1024, 512, 512
+UNIT_ROWS = 512
+ROW_TILES = UNIT_ROWS // P
+UNITS_PER_BATCH = Q_ROWS // UNIT_ROWS
+UNITS = BATCHES * UNITS_PER_BATCH
+PIECE_ROWS = C_ROWS // UNITS_PER_BATCH
+PIECE_TILES = PIECE_ROWS // P
+MASK_PENALTY = 10000.0
+
+FLOPS = 2 * BATCHES * Q_ROWS * FEATURES * FEATURES + 2 * BATCHES * Q_ROWS * C_ROWS * FEATURES
+
+
+def tile_attention_pa_t_kernel(
+    tc, query, context, query_bit, context_bit, W_in_words, W_in_scales, b_in, out
+):
+    nc = tc.nc
+    with ExitStack() as stack:
+        stack.enter_context(tc.manual_schedule())
+        const = stack.enter_context(tc.tile_pool(name="const", bufs=1))
+        work = stack.enter_context(tc.tile_pool(name="work", bufs=2))
+        result = stack.enter_context(tc.tile_pool(name="result", bufs=5))
+        turn_banks = stack.enter_context(tc.psum_pool(name="turn_banks", bufs=2))
+        q_banks = stack.enter_context(tc.psum_pool(name="q_banks", bufs=3))
+        score_banks = stack.enter_context(tc.psum_pool(name="score_banks", bufs=3))
+
+        bias_rows = const.tile([P, P], BF16, name="bias_rows")
+        nc.vector.memset(bias_rows[:], 0.0)
+        nc.sync.dma_start(out=bias_rows[0:PACK, :], in_=b_in.rearrange("(t p) -> t p", p=P))
+
+        x_raw = {}
+        c_raw = {}
+
+        def load_unit(u):
+            b, h = divmod(u, UNITS_PER_BATCH)
+            x_raw[u] = const.tile([P, ROW_TILES, FEATURES], BF16, name="x_raw%d" % u)
+            rows = query[b, h * UNIT_ROWS : (h + 1) * UNIT_ROWS, :]
+            nc.sync.dma_start(out=x_raw[u][:], in_=rows.rearrange("(p r) k -> p r k", r=ROW_TILES))
+            c_raw[u] = const.tile([P, PIECE_TILES, FEATURES], BF16, name="c_raw%d" % u)
+            rows = context[b, h * PIECE_ROWS : (h + 1) * PIECE_ROWS, :]
+            nc.sync.dma_start(out=c_raw[u][:], in_=rows.rearrange("(r p) d -> p r d", p=P))
+
+        load_unit(0)
+
+        w_scales = const.tile([P, FEATURES], U8, name="w_scales", align_bytes=64)
+        nc.vector.memset(w_scales[:].bitcast(I32), 0)
+        for quadrant in range(4):
+            nc.sync.dma_start(
+                out=w_scales[32 * quadrant : 32 * quadrant + 4, :].bitcast(I32),
+                in_=W_in_scales[0, 4 * quadrant : 4 * quadrant + 4, :].bitcast(I32),
+            )
+        w_words = const.tile([P, FEATURES], U32, name="w_words", align_bytes=64)
+        nc.sync.dma_start(
+            out=w_words[:].bitcast(I32),
+            in_=W_in_words.rearrange("g p n t -> (g p) (n t)").bitcast(I32),
+        )
+
+        load_unit(1)
+
+        qbit_raw = const.tile([P, UNITS, ROW_TILES], BF16, name="qbit_raw")
+        nc.sync.dma_start(
+            out=qbit_raw[:],
+            in_=query_bit.rearrange("b (h p r) -> p (b h) r", p=P, r=ROW_TILES),
+        )
+        cbit_raw = const.tile([P, BATCHES * C_ROWS], BF16, name="cbit_raw")
+        nc.sync.dma_start(
+            out=cbit_raw[:], in_=context_bit.rearrange("b j -> (b j)").partition_broadcast(P)
+        )
+        for u in range(2, UNITS):
+            load_unit(u)
+
+        ident_f32 = const.tile([P, P], F32, name="ident_f32")
+        make_identity(nc, ident_f32[:])
+        ident_bf16 = const.tile([P, P], BF16, name="ident_bf16")
+        make_identity(nc, ident_bf16[:])
+
+        bias_turned = turn_banks.tile([P, P], BF16, name="bias_turned", tag="turned")
+        nc.tensor.transpose(out=bias_turned[:], in_=bias_rows[:], identity=ident_bf16[:])
+        bias_cols = const.tile([P, PACK], F32, name="bias_cols")
+        nc.vector.tensor_copy(out=bias_cols[:], in_=bias_turned[:, 0:PACK])
+
+        mask_weight = const.tile([P, UNITS * ROW_TILES], F32, name="mask_weight")
+        cbit_minus_1 = const.tile([P, BATCHES, C_ROWS], BF16, name="cbit_minus_1")
+
+        def prepare_mask():
+            nc.vector.tensor_scalar_mul(
+                out=mask_weight[:], in0=qbit_raw[:].rearrange("p u r -> p (u r)"), scalar1=MASK_PENALTY
+            )
+            nc.vector.tensor_scalar_add(
+                out=cbit_minus_1[:].rearrange("p b j -> p (b j)"), in0=cbit_raw[:], scalar1=-1.0
+            )
+
+        x_turned, c_turned, x_grouped, c_grouped = {}, {}, {}, {}
+        x_words, x_scales, c_words, c_scales = {}, {}, {}, {}
+        q_sums, q_planes, q_grouped, q_words, q_scales = {}, {}, {}, {}, {}
+        score_sums, probs, neg_max, row_sum, inv_sum = {}, {}, {}, {}, {}
+
+        def turn_query_rows(u, pair):
+            turned = turn_banks.tile([P, 2, 2, P], F32, name="x_turned", tag="turned")
+            x_turned[u, pair] = turned
+            for rr in range(2):
+                words = x_raw[u][:, 2 * pair + rr, :].bitcast(F32)
+                for half in range(2):
+                    nc.tensor.transpose(
+                        out=turned[:, rr, half, :],
+                        in_=words[:, half : FEATURES // 2 : 2],
+                        identity=ident_f32[:],
+                    )
+
+        def turn_context_rows(u):
+            turned = turn_banks.tile([P, PIECE_TILES, PACK, P], BF16, name="c_turned", tag="turned")
+            c_turned[u] = turned
+            for rr in range(PIECE_TILES):
+                for t in range(PACK):
+                    nc.tensor.transpose(
+                        out=turned[:, rr, t, :],
+                        in_=c_raw[u][:, rr, t * P : (t + 1) * P],
+                        identity=ident_bf16[:],
+                    )
+
+        def front_transposes(u):
+            turn_query_rows(u, 0)
+            turn_context_rows(u)
+            turn_query_rows(u, 1)
+
+        def copy_query_rows(u, pair):
+            as_words = x_grouped[u][:].rearrange("p c t -> p (c t)").bitcast(F32)
+            as_words = as_words.rearrange("p (pair r i half) -> p pair r i half", r=2, i=P, half=2)
+            nc.scalar.copy(
+                out=as_words[:, pair], in_=x_turned[u, pair][:].rearrange("p r half i -> p r i half")
+            )
+
+        def copy_context_rows(u):
+            nc.scalar.copy(
+                out=c_grouped[u][:].rearrange("p (r j) t -> p r j t", j=P),
+                in_=c_turned[u][:].rearrange("p r t j -> p r j t"),
+            )
+
+        def front_copies(u):
+            x_grouped[u] = work.tile([P, UNIT_ROWS, PACK], BF16, name="x_grouped", align_bytes=64)
+            c_grouped[u] = work.tile([P, PIECE_ROWS, PACK], BF16, name="c_grouped", align_bytes=64)
+            copy_query_rows(u, 0)
+            copy_context_rows(u)
+            copy_query_rows(u, 1)
+
+        def quantise_query(u):
+            x_words[u] = work.tile([P, UNIT_ROWS], U32, name="x_words", align_bytes=64)
+            x_scales[u] = work.tile([P, UNIT_ROWS], U8, name="x_scales", align_bytes=64)
+            nc.vector.quantize_mx(
+                out=x_words[u][:].bitcast(FP8X4),
+                scales=x_scales[u][:],
+                in_=x_grouped[u][:].rearrange("p c t -> p (c t)"),
+            )
+
+        def quantise_context(u):
+            b, h = divmod(u, UNITS_PER_BATCH)
+            if h == 0:
+                c_words[b] = work.tile([P, C_ROWS], U32, name="c_words", align_bytes=64)
+                c_scales[b] = work.tile([P, C_ROWS], U8, name="c_scales", align_bytes=64)
+            piece = slice(h * PIECE_ROWS, (h + 1) * PIECE_ROWS)
+            nc.vector.quantize_mx(
+                out=c_words[b][:, piece].bitcast(FP8X4),
+                scales=c_scales[b][:, piece],
+                in_=c_grouped[u][:].rearrange("p j t -> p (j t)"),
+            )
+
+        def mid_matmuls(u):
+            for t in range(PACK):
+                sums = q_banks.tile([P, UNIT_ROWS], F32, name="q_sums")
+                q_sums[u, t] = sums
+                nc.tensor.matmul_mx(
+                    out=sums[:],
+                    lhsT=w_words[:, t * P : (t + 1) * P].bitcast(FP8X4),
+                    lhsT_scale=w_scales[:, t * P : (t + 1) * P],
+                    rhs=x_words[u][:].bitcast(FP8X4),
+                    rhs_scale=x_scales[u][:],
+                    start=True,
+                    stop=True,
+                )
+
+        def mid_bias(u):
+            q_planes[u] = work.tile([P, PACK, UNIT_ROWS], BF16, name="q_planes")
+            for t in range(PACK):
+                nc.scalar.activation(
+                    out=q_planes[u][:, t, :],
+                    in_=q_sums[u, t][:],
+                    func=ACT.Identity,
+                    bias=bias_cols[:, t : t + 1],
+                    scale=1.0,
+                )
+
+        def mid_regroup(u):
+            q_grouped[u] = work.tile([P, UNIT_ROWS, PACK], BF16, name="q_grouped", align_bytes=64)
+            nc.vector.tensor_copy(
+                out=q_grouped[u][:].rearrange("p (c i) t -> p c t i", i=4),
+                in_=q_planes[u][:].rearrange("p t (c i) -> p c t i", i=4),
+            )
+
+        def mid_quantise(u):
+            q_words[u] = work.tile([P, UNIT_ROWS], U32, name="q_words", align_bytes=64)
+            q_scales[u] = work.tile([P, UNIT_ROWS], U8, name="q_scales", align_bytes=64)
+            nc.vector.quantize_mx(
+                out=q_words[u][:].bitcast(FP8X4),
+                scales=q_scales[u][:],
+                in_=q_grouped[u][:].rearrange("p c t -> p (c t)"),
+            )
+
+        def back_matmuls(u):
+            b = u // UNITS_PER_BATCH
+            for r in range(ROW_TILES):
+                sums = score_banks.tile([P, C_ROWS], F32, name="score_sums")
+                score_sums[u, r] = sums
+                nc.tensor.matmul_mx(
+                    out=sums[:],
+                    lhsT=q_words[u][:, r * P : (r + 1) * P].bitcast(FP8X4),
+                    lhsT_scale=q_scales[u][:, r * P : (r + 1) * P],
+                    rhs=c_words[b][:].bitcast(FP8X4),
+                    rhs_scale=c_scales[b][:],
+                    start=True,
+                    stop=True,
+                )
+
+        def add_mask(u, r):
+            nc.vector.scalar_tensor_tensor(
+                out=probs[u][:, r, :],
+                in0=cbit_minus_1[:, u // UNITS_PER_BATCH, :],
+                scalar=mask_weight[:, u * ROW_TILES + r : u * ROW_TILES + r + 1],
+                in1=score_sums[u, r][:],
+                op0=ALU.mult,
+                op1=ALU.add,
+            )
+
+        def row_maximum(u, r):
+            nc.vector.tensor_reduce(
+                out=neg_max[u][:, r : r + 1], in_=probs[u][:, r, :], axis=AXIS.X, op=ALU.max, negate=True
+            )
+
+        def back_mask_and_maximum(u):
+            probs[u] = result.tile([P, ROW_TILES, C_ROWS], F32, name="probs")
+            neg_max[u] = result.tile([P, ROW_TILES], F32, name="neg_max")
+            for r in range(ROW_TILES):
+                add_mask(u, r)
+                if r > 0:
+                    row_maximum(u, r - 1)
+            row_maximum(u, ROW_TILES - 1)
+
+        def back_exp(u):
+            row_sum[u] = result.tile([P, ROW_TILES], F32, name="row_sum")
+            for r in range(ROW_TILES):
+                nc.scalar.activation(
+                    out=probs[u][:, r, :],
+                    in_=probs[u][:, r, :],
+                    func=ACT.Exp,
+                    bias=neg_max[u][:, r : r + 1],
+                    scale=1.0,
+                    accum_out=row_sum[u][:, r : r + 1],
+                )
+
+        def back_reciprocal(u):
+            inv_sum[u] = result.tile([P, ROW_TILES], F32, name="inv_sum")
+            nc.vector.reciprocal(out=inv_sum[u][:], in_=row_sum[u][:])
+
+        def back_divide_and_store(u):
+            engine = nc.vector if u >= UNITS - 2 else nc.gpsimd
+            b, h = divmod(u, UNITS_PER_BATCH)
+            rows = out[b, h * UNIT_ROWS : (h + 1) * UNIT_ROWS, :].rearrange("(p r) j -> p r j", r=ROW_TILES)
+            for r in range(ROW_TILES):
+                engine.tensor_scalar(
+                    out=probs[u][:, r, :],
+                    in0=probs[u][:, r, :],
+                    scalar1=inv_sum[u][:, r : r + 1],
+                    scalar2=0.0,
+                    op0=ALU.mult,
+                    op1=ALU.add,
+                )
+                nc.sync.dma_start(out=rows[:, r, :], in_=probs[u][:, r, :])
+
+        def exists(u):
+            return 0 <= u < UNITS
+
+        for step in range(-3, UNITS + 2):
+            leaving, in_back, in_mid, to_quantise, in_front = step - 2, step, step + 1, step + 2, step + 3
+            if exists(leaving):
+                back_reciprocal(leaving)
+                back_divide_and_store(leaving)
+            if exists(in_back):
+                back_matmuls(in_back)
+            if exists(in_mid):
+                mid_matmuls(in_mid)
+            if exists(in_front):
+                front_transposes(in_front)
+            if exists(in_mid):
+                mid_bias(in_mid)
+            if exists(in_back):
+                back_mask_and_maximum(in_back)
+            if exists(in_front):
+                front_copies(in_front)
+            if exists(in_back):
+                back_exp(in_back)
+            if exists(in_mid):
+                mid_regroup(in_mid)
+            if exists(to_quantise):
+                quantise_context(to_quantise)
+            if exists(in_mid):
+                mid_quantise(in_mid)
+            if exists(to_quantise):
+                quantise_query(to_quantise)
+            if to_quantise == 0:
+                prepare_mask()

@@ -36,9 +36,9 @@ def tile_attention_pa_t_kernel(
         const = stack.enter_context(tc.tile_pool(name="const", bufs=1))
         work = stack.enter_context(tc.tile_pool(name="work", bufs=2))
         result = stack.enter_context(tc.tile_pool(name="result", bufs=5))
-        turn_banks = stack.enter_context(tc.psum_pool(name="turn_banks", bufs=2))
+        turn_banks = stack.enter_context(tc.psum_pool(name="turn_banks", bufs=3))
         q_banks = stack.enter_context(tc.psum_pool(name="q_banks", bufs=3))
-        score_banks = stack.enter_context(tc.psum_pool(name="score_banks", bufs=3))
+        score_banks = stack.enter_context(tc.psum_pool(name="score_banks", bufs=2))
 
         bias_rows = const.tile([P, P], BF16, name="bias_rows")
         nc.vector.memset(bias_rows[:], 0.0)
@@ -136,8 +136,8 @@ def tile_attention_pa_t_kernel(
 
         def front_transposes(u):
             turn_query_rows(u, 0)
-            turn_context_rows(u)
             turn_query_rows(u, 1)
+            turn_context_rows(u)
 
         def copy_query_rows(u, pair):
             as_words = x_grouped[u][:].rearrange("p c t -> p (c t)").bitcast(F32)
@@ -156,8 +156,8 @@ def tile_attention_pa_t_kernel(
             x_grouped[u] = work.tile([P, UNIT_ROWS, PACK], BF16, name="x_grouped", align_bytes=64)
             c_grouped[u] = work.tile([P, PIECE_ROWS, PACK], BF16, name="c_grouped", align_bytes=64)
             copy_query_rows(u, 0)
-            copy_context_rows(u)
             copy_query_rows(u, 1)
+            copy_context_rows(u)
 
         def quantise_query(u):
             x_words[u] = work.tile([P, UNIT_ROWS], U32, name="x_words", align_bytes=64)
@@ -254,11 +254,11 @@ def tile_attention_pa_t_kernel(
         def back_mask_and_maximum(u):
             probs[u] = result.tile([P, ROW_TILES, C_ROWS], F32, name="probs")
             neg_max[u] = result.tile([P, ROW_TILES], F32, name="neg_max")
-            for r in range(ROW_TILES):
+            for r in range(0, ROW_TILES, 2):
                 add_mask(u, r)
-                if r > 0:
-                    row_maximum(u, r - 1)
-            row_maximum(u, ROW_TILES - 1)
+                add_mask(u, r + 1)
+                row_maximum(u, r)
+                row_maximum(u, r + 1)
 
         def back_exp(u):
             row_sum[u] = result.tile([P, ROW_TILES], F32, name="row_sum")
@@ -294,32 +294,29 @@ def tile_attention_pa_t_kernel(
         def exists(u):
             return 0 <= u < UNITS
 
-        for step in range(-3, UNITS + 2):
-            leaving, in_back, in_mid, to_quantise, in_front = step - 2, step, step + 1, step + 2, step + 3
-            if exists(leaving):
-                back_reciprocal(leaving)
-                back_divide_and_store(leaving)
-            if exists(in_back):
-                back_matmuls(in_back)
-            if exists(in_mid):
-                mid_matmuls(in_mid)
-            if exists(in_front):
-                front_transposes(in_front)
-            if exists(in_mid):
-                mid_bias(in_mid)
-            if exists(in_back):
-                back_mask_and_maximum(in_back)
-            if exists(in_front):
-                front_copies(in_front)
-            if exists(in_back):
-                back_exp(in_back)
-            if exists(in_mid):
-                mid_regroup(in_mid)
-            if exists(to_quantise):
-                quantise_context(to_quantise)
-            if exists(in_mid):
-                mid_quantise(in_mid)
-            if exists(to_quantise):
-                quantise_query(to_quantise)
-            if to_quantise == 0:
+        for step in range(-4, UNITS + 2):
+            if exists(step - 2):
+                back_reciprocal(step - 2)
+                back_divide_and_store(step - 2)
+            if exists(step + 2):
+                mid_matmuls(step + 2)
+            if exists(step + 4):
+                front_transposes(step + 4)
+            if exists(step):
+                back_mask_and_maximum(step)
+            if exists(step + 3):
+                front_copies(step + 3)
+            if exists(step + 2):
+                mid_bias(step + 2)
+            if exists(step):
+                back_exp(step)
+            if exists(step + 1):
+                mid_quantise(step + 1)
+                back_matmuls(step + 1)
+            if exists(step + 3):
+                quantise_context(step + 3)
+                quantise_query(step + 3)
+            if exists(step + 2):
+                mid_regroup(step + 2)
+            if step + 3 == 0:
                 prepare_mask()

@@ -23,6 +23,7 @@ UNITS = BATCHES * UNITS_PER_BATCH
 PIECE_ROWS = C_ROWS // UNITS_PER_BATCH
 PIECE_TILES = PIECE_ROWS // P
 MASK_PENALTY = 10000.0
+TURN_BANKS, Q_BANKS, SCORE_BANKS = 3, 3, 2
 
 FLOPS = 2 * BATCHES * Q_ROWS * FEATURES * FEATURES + 2 * BATCHES * Q_ROWS * C_ROWS * FEATURES
 
@@ -36,9 +37,9 @@ def tile_attention_pa_t_kernel(
         const = stack.enter_context(tc.tile_pool(name="const", bufs=1))
         work = stack.enter_context(tc.tile_pool(name="work", bufs=2))
         result = stack.enter_context(tc.tile_pool(name="result", bufs=5))
-        turn_banks = stack.enter_context(tc.psum_pool(name="turn_banks", bufs=3))
-        q_banks = stack.enter_context(tc.psum_pool(name="q_banks", bufs=3))
-        score_banks = stack.enter_context(tc.psum_pool(name="score_banks", bufs=2))
+        turn_banks = stack.enter_context(tc.psum_pool(name="turn_banks", bufs=TURN_BANKS))
+        q_banks = stack.enter_context(tc.psum_pool(name="q_banks", bufs=Q_BANKS))
+        score_banks = stack.enter_context(tc.psum_pool(name="score_banks", bufs=SCORE_BANKS))
 
         bias_rows = const.tile([P, P], BF16, name="bias_rows")
         nc.vector.memset(bias_rows[:], 0.0)
@@ -71,7 +72,8 @@ def tile_attention_pa_t_kernel(
             in_=W_in_words.rearrange("g p n t -> (g p) (n t)").bitcast(I32),
         )
 
-        load_unit(1)
+        for u in range(1, 4):
+            load_unit(u)
 
         qbit_raw = const.tile([P, UNITS, ROW_TILES], BF16, name="qbit_raw")
         nc.sync.dma_start(
@@ -82,7 +84,7 @@ def tile_attention_pa_t_kernel(
         nc.sync.dma_start(
             out=cbit_raw[:], in_=context_bit.rearrange("b j -> (b j)").partition_broadcast(P)
         )
-        for u in range(2, UNITS):
+        for u in range(4, UNITS):
             load_unit(u)
 
         ident_f32 = const.tile([P, P], F32, name="ident_f32")
@@ -180,8 +182,8 @@ def tile_attention_pa_t_kernel(
                 in_=c_grouped[u][:].rearrange("p j t -> p (j t)"),
             )
 
-        def mid_matmuls(u):
-            for t in range(PACK):
+        def mid_matmuls(u, planes):
+            for t in planes:
                 sums = q_banks.tile([P, UNIT_ROWS], F32, name="q_sums")
                 q_sums[u, t] = sums
                 nc.tensor.matmul_mx(
@@ -221,9 +223,9 @@ def tile_attention_pa_t_kernel(
                 in_=q_grouped[u][:].rearrange("p c t -> p (c t)"),
             )
 
-        def back_matmuls(u):
+        def back_matmuls(u, row_tiles):
             b = u // UNITS_PER_BATCH
-            for r in range(ROW_TILES):
+            for r in row_tiles:
                 sums = score_banks.tile([P, C_ROWS], F32, name="score_sums")
                 score_sums[u, r] = sums
                 nc.tensor.matmul_mx(
@@ -299,7 +301,11 @@ def tile_attention_pa_t_kernel(
                 back_reciprocal(step - 2)
                 back_divide_and_store(step - 2)
             if exists(step + 2):
-                mid_matmuls(step + 2)
+                mid_matmuls(step + 2, range(0, Q_BANKS))
+            if exists(step):
+                back_matmuls(step, range(SCORE_BANKS, ROW_TILES))
+            if exists(step + 2):
+                mid_matmuls(step + 2, range(Q_BANKS, PACK))
             if exists(step + 4):
                 front_transposes(step + 4)
             if exists(step):
@@ -312,7 +318,7 @@ def tile_attention_pa_t_kernel(
                 back_exp(step)
             if exists(step + 1):
                 mid_quantise(step + 1)
-                back_matmuls(step + 1)
+                back_matmuls(step + 1, range(0, SCORE_BANKS))
             if exists(step + 3):
                 quantise_context(step + 3)
                 quantise_query(step + 3)

@@ -72,17 +72,16 @@ def tile_attention_pa_t_kernel(
             in_=W_in_words.rearrange("g p n t -> (g p) (n t)").bitcast(I32),
         )
 
+        cbit_rows = const.tile([P, C_ROWS], BF16, name="cbit_rows")
+        nc.vector.memset(cbit_rows[:], 0.0)
+        nc.sync.dma_start(out=cbit_rows[0:BATCHES, :], in_=context_bit)
+
         for u in range(1, 4):
             load_unit(u)
-
         qbit_raw = const.tile([P, UNITS, ROW_TILES], BF16, name="qbit_raw")
         nc.sync.dma_start(
             out=qbit_raw[:],
             in_=query_bit.rearrange("b (h p r) -> p (b h) r", p=P, r=ROW_TILES),
-        )
-        cbit_raw = const.tile([P, BATCHES * C_ROWS], BF16, name="cbit_raw")
-        nc.sync.dma_start(
-            out=cbit_raw[:], in_=context_bit.rearrange("b j -> (b j)").partition_broadcast(P)
         )
         for u in range(4, UNITS):
             load_unit(u)
@@ -100,12 +99,26 @@ def tile_attention_pa_t_kernel(
         mask_weight = const.tile([P, UNITS * ROW_TILES], F32, name="mask_weight")
         cbit_minus_1 = const.tile([P, BATCHES, C_ROWS], BF16, name="cbit_minus_1")
 
-        def prepare_mask():
+        cbit_spread = {}
+
+        def prepare_mask_weight():
             nc.vector.tensor_scalar_mul(
                 out=mask_weight[:], in0=qbit_raw[:].rearrange("p u r -> p (u r)"), scalar1=MASK_PENALTY
             )
-            nc.vector.tensor_scalar_add(
-                out=cbit_minus_1[:].rearrange("p b j -> p (b j)"), in0=cbit_raw[:], scalar1=-1.0
+
+        def spread_context_bits(b):
+            cbit_spread[b] = q_banks.tile([P, C_ROWS], F32, name="cbit_spread", tag="q_sums")
+            nc.tensor.matmul(
+                out=cbit_spread[b][:],
+                lhsT=ident_bf16[:, b : b + 1].to_broadcast([P, P]),
+                rhs=cbit_rows[:],
+                start=True,
+                stop=True,
+            )
+
+        def copy_context_bits(b):
+            nc.scalar.activation(
+                out=cbit_minus_1[:, b, :], in_=cbit_spread[b][:], func=ACT.Copy, bias=-1.0, scale=1.0
             )
 
         x_turned, c_turned, x_grouped, c_grouped = {}, {}, {}, {}
@@ -296,6 +309,9 @@ def tile_attention_pa_t_kernel(
         def exists(u):
             return 0 <= u < UNITS
 
+        def starts_batch(u):
+            return exists(u) and u % UNITS_PER_BATCH == 0
+
         for step in range(-4, UNITS + 2):
             if exists(step - 2):
                 back_reciprocal(step - 2)
@@ -306,6 +322,8 @@ def tile_attention_pa_t_kernel(
                 back_matmuls(step, range(SCORE_BANKS, ROW_TILES))
             if exists(step + 2):
                 mid_matmuls(step + 2, range(Q_BANKS, PACK))
+            if starts_batch(step + 2):
+                spread_context_bits((step + 2) // UNITS_PER_BATCH)
             if exists(step + 4):
                 front_transposes(step + 4)
             if exists(step):
@@ -314,6 +332,8 @@ def tile_attention_pa_t_kernel(
                 front_copies(step + 3)
             if exists(step + 2):
                 mid_bias(step + 2)
+            if starts_batch(step + 2):
+                copy_context_bits((step + 2) // UNITS_PER_BATCH)
             if exists(step):
                 back_exp(step)
             if exists(step + 1):
@@ -322,7 +342,7 @@ def tile_attention_pa_t_kernel(
             if exists(step + 3):
                 quantise_context(step + 3)
                 quantise_query(step + 3)
+            if step + 1 == 0:
+                prepare_mask_weight()
             if exists(step + 2):
                 mid_regroup(step + 2)
-            if step + 3 == 0:
-                prepare_mask()

@@ -22,6 +22,7 @@ UNITS_PER_BATCH = Q_ROWS // UNIT_ROWS
 UNITS = BATCHES * UNITS_PER_BATCH
 PIECE_ROWS = C_ROWS // UNITS_PER_BATCH
 PIECE_TILES = PIECE_ROWS // P
+GPSIMD_ROWS = 384
 MASK_PENALTY = 10000.0
 TURN_BANKS, Q_BANKS, SCORE_BANKS = 3, 3, 2
 
@@ -220,11 +221,21 @@ def tile_attention_pa_t_kernel(
                     scale=1.0,
                 )
 
-        def mid_regroup(u):
+        def mid_regroup_vector(u):
             q_grouped[u] = work.tile([P, UNIT_ROWS, PACK], BF16, name="q_grouped", align_bytes=64)
             nc.vector.tensor_copy(
-                out=q_grouped[u][:].rearrange("p (c i) t -> p c t i", i=4),
-                in_=q_planes[u][:].rearrange("p t (c i) -> p c t i", i=4),
+                out=q_grouped[u][:, GPSIMD_ROWS:, :].rearrange("p (c i) t -> p c t i", i=4),
+                in_=q_planes[u][:, :, GPSIMD_ROWS:].rearrange("p t (c i) -> p c t i", i=4),
+            )
+
+        def mid_regroup_gpsimd(u):
+            nc.gpsimd.tensor_scalar(
+                out=q_grouped[u][:, 0:GPSIMD_ROWS, :],
+                in0=q_planes[u][:, :, 0:GPSIMD_ROWS].rearrange("p t c -> p c t"),
+                scalar1=1.0,
+                scalar2=0.0,
+                op0=ALU.mult,
+                op1=ALU.add,
             )
 
         def mid_quantise(u):
@@ -313,6 +324,8 @@ def tile_attention_pa_t_kernel(
             return exists(u) and u % UNITS_PER_BATCH == 0
 
         for step in range(-4, UNITS + 2):
+            if exists(step + 1):
+                mid_regroup_gpsimd(step + 1)
             if exists(step - 2):
                 back_reciprocal(step - 2)
                 back_divide_and_store(step - 2)
@@ -345,4 +358,4 @@ def tile_attention_pa_t_kernel(
             if step + 1 == 0:
                 prepare_mask_weight()
             if exists(step + 2):
-                mid_regroup(step + 2)
+                mid_regroup_vector(step + 2)

@@ -42,9 +42,9 @@ def tile_attention_pa_t_kernel(
         q_banks = stack.enter_context(tc.psum_pool(name="q_banks", bufs=Q_BANKS))
         score_banks = stack.enter_context(tc.psum_pool(name="score_banks", bufs=SCORE_BANKS))
 
-        bias_rows = const.tile([P, P], BF16, name="bias_rows")
-        nc.vector.memset(bias_rows[:], 0.0)
-        nc.sync.dma_start(out=bias_rows[0:PACK, :], in_=b_in.rearrange("(t p) -> t p", p=P))
+        bias_row = const.tile([P, FEATURES], BF16, name="bias_row")
+        nc.vector.memset(bias_row[:], 0.0)
+        nc.sync.dma_start(out=bias_row[0:1, :], in_=b_in.rearrange("(o n) -> o n", o=1))
 
         x_raw = {}
         c_raw = {}
@@ -60,16 +60,16 @@ def tile_attention_pa_t_kernel(
 
         load_unit(0)
 
-        w_scales = const.tile([P, FEATURES], U8, name="w_scales", align_bytes=64)
-        nc.vector.memset(w_scales[:].bitcast(I32), 0)
+        w_scales_raw = const.tile([P, FEATURES], U8, name="w_scales_raw", align_bytes=64)
+        nc.vector.memset(w_scales_raw[:].bitcast(I32), 0)
         for quadrant in range(4):
             nc.sync.dma_start(
-                out=w_scales[32 * quadrant : 32 * quadrant + 4, :].bitcast(I32),
+                out=w_scales_raw[32 * quadrant : 32 * quadrant + 4, :].bitcast(I32),
                 in_=W_in_scales[0, 4 * quadrant : 4 * quadrant + 4, :].bitcast(I32),
             )
-        w_words = const.tile([P, FEATURES], U32, name="w_words", align_bytes=64)
+        w_words_raw = const.tile([P, FEATURES], U32, name="w_words_raw", align_bytes=64)
         nc.sync.dma_start(
-            out=w_words[:].bitcast(I32),
+            out=w_words_raw[:].bitcast(I32),
             in_=W_in_words.rearrange("g p n t -> (g p) (n t)").bitcast(I32),
         )
 
@@ -92,10 +92,26 @@ def tile_attention_pa_t_kernel(
         ident_bf16 = const.tile([P, P], BF16, name="ident_bf16")
         make_identity(nc, ident_bf16[:])
 
-        bias_turned = turn_banks.tile([P, P], BF16, name="bias_turned", tag="turned")
-        nc.tensor.transpose(out=bias_turned[:], in_=bias_rows[:], identity=ident_bf16[:])
+        bias_turned = turn_banks.tile([P, PACK, P], BF16, name="bias_turned", tag="turned")
+        for t in range(PACK):
+            nc.tensor.transpose(
+                out=bias_turned[:, t, :], in_=bias_row[:, t:FEATURES:PACK], identity=ident_bf16[:]
+            )
         bias_cols = const.tile([P, PACK], F32, name="bias_cols")
-        nc.vector.tensor_copy(out=bias_cols[:], in_=bias_turned[:, 0:PACK])
+        nc.vector.tensor_copy(out=bias_cols[:], in_=bias_turned[:, :, 0])
+
+        w_words = const.tile([P, FEATURES], U32, name="w_words", align_bytes=64)
+        w_scales = const.tile([P, FEATURES], U8, name="w_scales", align_bytes=64)
+
+        def order_weights():
+            nc.vector.tensor_copy(
+                out=w_words[:].bitcast(I32).rearrange("p (t m) -> p m t", t=PACK),
+                in_=w_words_raw[:].bitcast(I32).rearrange("p (m t) -> p m t", t=PACK),
+            )
+            nc.vector.tensor_copy(
+                out=w_scales[:].rearrange("p (t m) -> p m t", t=PACK),
+                in_=w_scales_raw[:].rearrange("p (m t) -> p m t", t=PACK),
+            )
 
         mask_weight = const.tile([P, UNITS * ROW_TILES], F32, name="mask_weight")
         cbit_minus_1 = const.tile([P, BATCHES, C_ROWS], BF16, name="cbit_minus_1")
@@ -140,14 +156,15 @@ def tile_attention_pa_t_kernel(
                     )
 
         def turn_context_rows(u):
-            turned = turn_banks.tile([P, PIECE_TILES, PACK, P], BF16, name="c_turned", tag="turned")
+            turned = turn_banks.tile([P, PIECE_TILES, 2, P], F32, name="c_turned", tag="turned")
             c_turned[u] = turned
             for rr in range(PIECE_TILES):
-                for t in range(PACK):
+                words = c_raw[u][:, rr, :].bitcast(F32)
+                for half in range(2):
                     nc.tensor.transpose(
-                        out=turned[:, rr, t, :],
-                        in_=c_raw[u][:, rr, t * P : (t + 1) * P],
-                        identity=ident_bf16[:],
+                        out=turned[:, rr, half, :],
+                        in_=words[:, half : FEATURES // 2 : 2],
+                        identity=ident_f32[:],
                     )
 
         def front_transposes(u):
@@ -163,9 +180,10 @@ def tile_attention_pa_t_kernel(
             )
 
         def copy_context_rows(u):
+            as_words = c_grouped[u][:].rearrange("p j t -> p (j t)").bitcast(F32)
             nc.scalar.copy(
-                out=c_grouped[u][:].rearrange("p (r j) t -> p r j t", j=P),
-                in_=c_turned[u][:].rearrange("p r t j -> p r j t"),
+                out=as_words.rearrange("p (r j half) -> p r j half", j=P, half=2),
+                in_=c_turned[u][:].rearrange("p r half j -> p r j half"),
             )
 
         def front_copies(u):
@@ -352,9 +370,11 @@ def tile_attention_pa_t_kernel(
             if exists(step + 1):
                 mid_quantise(step + 1)
                 back_matmuls(step + 1, range(0, SCORE_BANKS))
+            if step + 3 == 0:
+                order_weights()
             if exists(step + 3):
-                quantise_context(step + 3)
                 quantise_query(step + 3)
+                quantise_context(step + 3)
             if step + 1 == 0:
                 prepare_mask_weight()
             if exists(step + 2):

@@ -42,23 +42,22 @@ def tile_attention_pa_t_kernel(
         q_banks = stack.enter_context(tc.psum_pool(name="q_banks", bufs=Q_BANKS))
         score_banks = stack.enter_context(tc.psum_pool(name="score_banks", bufs=SCORE_BANKS))
 
-        bias_row = const.tile([P, FEATURES], BF16, name="bias_row")
-        nc.vector.memset(bias_row[:], 0.0)
-        nc.sync.dma_start(out=bias_row[0:1, :], in_=b_in.rearrange("(o n) -> o n", o=1))
-
         x_raw = {}
         c_raw = {}
 
-        def load_unit(u):
+        def load_query_rows(u, pieces=1):
             b, h = divmod(u, UNITS_PER_BATCH)
             x_raw[u] = const.tile([P, ROW_TILES, FEATURES], BF16, name="x_raw%d" % u)
-            rows = query[b, h * UNIT_ROWS : (h + 1) * UNIT_ROWS, :]
-            nc.sync.dma_start(out=x_raw[u][:], in_=rows.rearrange("(p r) k -> p r k", r=ROW_TILES))
+            rows = query[b, h * UNIT_ROWS : (h + 1) * UNIT_ROWS, :].rearrange("(p r) k -> p r k", r=ROW_TILES)
+            step = ROW_TILES // pieces
+            for r in range(0, ROW_TILES, step):
+                nc.sync.dma_start(out=x_raw[u][:, r : r + step, :], in_=rows[:, r : r + step, :])
+
+        def load_context_rows(u):
+            b, h = divmod(u, UNITS_PER_BATCH)
             c_raw[u] = const.tile([P, PIECE_TILES, FEATURES], BF16, name="c_raw%d" % u)
             rows = context[b, h * PIECE_ROWS : (h + 1) * PIECE_ROWS, :]
             nc.sync.dma_start(out=c_raw[u][:], in_=rows.rearrange("(r p) d -> p r d", p=P))
-
-        load_unit(0)
 
         w_scales_raw = const.tile([P, FEATURES], U8, name="w_scales_raw", align_bytes=64)
         nc.vector.memset(w_scales_raw[:].bitcast(I32), 0)
@@ -67,76 +66,87 @@ def tile_attention_pa_t_kernel(
                 out=w_scales_raw[32 * quadrant : 32 * quadrant + 4, :].bitcast(I32),
                 in_=W_in_scales[0, 4 * quadrant : 4 * quadrant + 4, :].bitcast(I32),
             )
+        load_query_rows(0, pieces=2)
+
         w_words_raw = const.tile([P, FEATURES], U32, name="w_words_raw", align_bytes=64)
         nc.sync.dma_start(
             out=w_words_raw[:].bitcast(I32),
             in_=W_in_words.rearrange("g p n t -> (g p) (n t)").bitcast(I32),
         )
 
+        row_inputs = const.tile([P, UNIT_ROWS], BF16, name="row_inputs")
+        nc.vector.memset(row_inputs[:], 0.0)
+        nc.sync.dma_start(
+            out=row_inputs[0:UNITS, :], in_=query_bit.rearrange("b (h i) -> (b h) i", i=UNIT_ROWS)
+        )
+        nc.sync.dma_start(out=row_inputs[UNITS : UNITS + 1, :], in_=b_in.rearrange("(o n) -> o n", o=1))
+
+        cbit_raw = const.tile([BATCHES, C_ROWS], BF16, name="cbit_raw")
+        nc.sync.dma_start(out=cbit_raw[:], in_=context_bit)
         cbit_rows = const.tile([P, C_ROWS], BF16, name="cbit_rows")
         nc.vector.memset(cbit_rows[:], 0.0)
-        nc.sync.dma_start(out=cbit_rows[0:BATCHES, :], in_=context_bit)
 
-        for u in range(1, 4):
-            load_unit(u)
-        qbit_raw = const.tile([P, UNITS, ROW_TILES], BF16, name="qbit_raw")
-        nc.sync.dma_start(
-            out=qbit_raw[:],
-            in_=query_bit.rearrange("b (h p r) -> p (b h) r", p=P, r=ROW_TILES),
-        )
-        for u in range(4, UNITS):
-            load_unit(u)
+        for u in range(UNITS_PER_BATCH):
+            load_context_rows(u)
+
+        load_query_rows(1)
+        for u in range(2, UNITS):
+            load_query_rows(u)
+            load_context_rows(u)
 
         ident_f32 = const.tile([P, P], F32, name="ident_f32")
         make_identity(nc, ident_f32[:])
         ident_bf16 = const.tile([P, P], BF16, name="ident_bf16")
         make_identity(nc, ident_bf16[:])
 
-        bias_turned = turn_banks.tile([P, PACK, P], BF16, name="bias_turned", tag="turned")
-        for t in range(PACK):
-            nc.tensor.transpose(
-                out=bias_turned[:, t, :], in_=bias_row[:, t:FEATURES:PACK], identity=ident_bf16[:]
-            )
+        mask_weight = const.tile([P, ROW_TILES, UNITS], F32, name="mask_weight")
         bias_cols = const.tile([P, PACK], F32, name="bias_cols")
-        nc.vector.tensor_copy(out=bias_cols[:], in_=bias_turned[:, :, 0])
+        cbit_minus_1 = const.tile([P, BATCHES, C_ROWS], BF16, name="cbit_minus_1")
 
         w_words = const.tile([P, FEATURES], U32, name="w_words", align_bytes=64)
         w_scales = const.tile([P, FEATURES], U8, name="w_scales", align_bytes=64)
 
-        def order_weights():
+        def order_weight_codes():
             nc.vector.tensor_copy(
                 out=w_words[:].bitcast(I32).rearrange("p (t m) -> p m t", t=PACK),
                 in_=w_words_raw[:].bitcast(I32).rearrange("p (m t) -> p m t", t=PACK),
             )
+
+        def order_weight_scales():
             nc.vector.tensor_copy(
                 out=w_scales[:].rearrange("p (t m) -> p m t", t=PACK),
                 in_=w_scales_raw[:].rearrange("p (m t) -> p m t", t=PACK),
             )
 
-        mask_weight = const.tile([P, UNITS * ROW_TILES], F32, name="mask_weight")
-        cbit_minus_1 = const.tile([P, BATCHES, C_ROWS], BF16, name="cbit_minus_1")
+        def prepare_small_inputs():
+            turned = turn_banks.tile([P, ROW_TILES, P], BF16, name="rows_turned", tag="turned")
+            for r in range(ROW_TILES):
+                nc.tensor.transpose(
+                    out=turned[:, r, :], in_=row_inputs[:, r:UNIT_ROWS:ROW_TILES], identity=ident_bf16[:]
+                )
+            nc.vector.tensor_copy(out=bias_cols[:], in_=turned[:, :, UNITS])
+            nc.vector.tensor_scalar_mul(
+                out=mask_weight[:], in0=turned[:, :, 0:UNITS], scalar1=MASK_PENALTY
+            )
+            nc.vector.tensor_scalar_add(out=cbit_rows[0:BATCHES, :], in0=cbit_raw[:], scalar1=-1.0)
 
         cbit_spread = {}
 
-        def prepare_mask_weight():
-            nc.vector.tensor_scalar_mul(
-                out=mask_weight[:], in0=qbit_raw[:].rearrange("p u r -> p (u r)"), scalar1=MASK_PENALTY
-            )
-
         def spread_context_bits(b):
-            cbit_spread[b] = q_banks.tile([P, C_ROWS], F32, name="cbit_spread", tag="q_sums")
-            nc.tensor.matmul(
-                out=cbit_spread[b][:],
-                lhsT=ident_bf16[:, b : b + 1].to_broadcast([P, P]),
-                rhs=cbit_rows[:],
-                start=True,
-                stop=True,
-            )
+            cbit_spread[b] = q_banks.tile([P, 2, C_ROWS], BF16, name="cbit_spread", tag="q_sums")
+            for i in range(2):
+                nc.tensor.matmul(
+                    out=cbit_spread[b][:, i, :],
+                    lhsT=ident_bf16[:, b + i : b + i + 1].to_broadcast([P, P]),
+                    rhs=cbit_rows[:],
+                    start=True,
+                    stop=True,
+                )
 
         def copy_context_bits(b):
-            nc.scalar.activation(
-                out=cbit_minus_1[:, b, :], in_=cbit_spread[b][:], func=ACT.Copy, bias=-1.0, scale=1.0
-            )
+            nc.scalar.copy(out=cbit_minus_1[:, b : b + 2, :], in_=cbit_spread[b][:])
+
+        last = UNITS - 1
 
         x_turned, c_turned, x_grouped, c_grouped = {}, {}, {}, {}
         x_words, x_scales, c_words, c_scales = {}, {}, {}, {}
@@ -172,14 +182,16 @@ def tile_attention_pa_t_kernel(
             turn_query_rows(u, 1)
             turn_context_rows(u)
 
-        def copy_query_rows(u, pair):
+        def copy_query_rows(u, pair, on_vector=False):
+            if pair == 0:
+                x_grouped[u] = work.tile([P, UNIT_ROWS, PACK], BF16, name="x_grouped", align_bytes=64)
+            copy = nc.vector.tensor_copy if on_vector else nc.scalar.copy
             as_words = x_grouped[u][:].rearrange("p c t -> p (c t)").bitcast(F32)
             as_words = as_words.rearrange("p (pair r i half) -> p pair r i half", r=2, i=P, half=2)
-            nc.scalar.copy(
-                out=as_words[:, pair], in_=x_turned[u, pair][:].rearrange("p r half i -> p r i half")
-            )
+            copy(out=as_words[:, pair], in_=x_turned[u, pair][:].rearrange("p r half i -> p r i half"))
 
         def copy_context_rows(u):
+            c_grouped[u] = work.tile([P, PIECE_ROWS, PACK], BF16, name="c_grouped", align_bytes=64)
             as_words = c_grouped[u][:].rearrange("p j t -> p (j t)").bitcast(F32)
             nc.scalar.copy(
                 out=as_words.rearrange("p (r j half) -> p r j half", j=P, half=2),
@@ -187,8 +199,6 @@ def tile_attention_pa_t_kernel(
             )
 
         def front_copies(u):
-            x_grouped[u] = work.tile([P, UNIT_ROWS, PACK], BF16, name="x_grouped", align_bytes=64)
-            c_grouped[u] = work.tile([P, PIECE_ROWS, PACK], BF16, name="c_grouped", align_bytes=64)
             copy_query_rows(u, 0)
             copy_query_rows(u, 1)
             copy_context_rows(u)
@@ -228,28 +238,34 @@ def tile_attention_pa_t_kernel(
                     stop=True,
                 )
 
-        def mid_bias(u):
-            q_planes[u] = work.tile([P, PACK, UNIT_ROWS], BF16, name="q_planes")
-            for t in range(PACK):
+        def mid_bias(u, t, on_vector=False):
+            if t == 0:
+                q_planes[u] = work.tile([P, PACK, UNIT_ROWS], BF16, name="q_planes")
+            bias = bias_cols[:, t : t + 1]
+            if on_vector:
+                nc.vector.tensor_scalar_add(out=q_planes[u][:, t, :], in0=q_sums[u, t][:], scalar1=bias)
+            else:
                 nc.scalar.activation(
-                    out=q_planes[u][:, t, :],
-                    in_=q_sums[u, t][:],
-                    func=ACT.Identity,
-                    bias=bias_cols[:, t : t + 1],
-                    scale=1.0,
+                    out=q_planes[u][:, t, :], in_=q_sums[u, t][:], func=ACT.Identity, bias=bias, scale=1.0
                 )
 
-        def mid_regroup_vector(u):
-            q_grouped[u] = work.tile([P, UNIT_ROWS, PACK], BF16, name="q_grouped", align_bytes=64)
+        def grouped_tile(u):
+            if u not in q_grouped:
+                q_grouped[u] = work.tile([P, UNIT_ROWS, PACK], BF16, name="q_grouped", align_bytes=64)
+            return q_grouped[u]
+
+        def mid_regroup_vector(u, first_row=GPSIMD_ROWS):
+            grouped = grouped_tile(u)
             nc.vector.tensor_copy(
-                out=q_grouped[u][:, GPSIMD_ROWS:, :].rearrange("p (c i) t -> p c t i", i=4),
-                in_=q_planes[u][:, :, GPSIMD_ROWS:].rearrange("p t (c i) -> p c t i", i=4),
+                out=grouped[:, first_row:, :].rearrange("p (c i) t -> p c t i", i=4),
+                in_=q_planes[u][:, :, first_row:].rearrange("p t (c i) -> p c t i", i=4),
             )
 
         def mid_regroup_gpsimd(u):
+            rows = UNIT_ROWS if u == last else GPSIMD_ROWS
             nc.gpsimd.tensor_scalar(
-                out=q_grouped[u][:, 0:GPSIMD_ROWS, :],
-                in0=q_planes[u][:, :, 0:GPSIMD_ROWS].rearrange("p t c -> p c t"),
+                out=grouped_tile(u)[:, 0:rows, :],
+                in0=q_planes[u][:, :, 0:rows].rearrange("p t c -> p c t"),
                 scalar1=1.0,
                 scalar2=0.0,
                 op0=ALU.mult,
@@ -280,11 +296,15 @@ def tile_attention_pa_t_kernel(
                     stop=True,
                 )
 
+        def start_back(u):
+            probs[u] = result.tile([P, ROW_TILES, C_ROWS], F32, name="probs")
+            neg_max[u] = result.tile([P, ROW_TILES], F32, name="neg_max")
+
         def add_mask(u, r):
             nc.vector.scalar_tensor_tensor(
                 out=probs[u][:, r, :],
                 in0=cbit_minus_1[:, u // UNITS_PER_BATCH, :],
-                scalar=mask_weight[:, u * ROW_TILES + r : u * ROW_TILES + r + 1],
+                scalar=mask_weight[:, r, u : u + 1],
                 in1=score_sums[u, r][:],
                 op0=ALU.mult,
                 op1=ALU.add,
@@ -295,18 +315,18 @@ def tile_attention_pa_t_kernel(
                 out=neg_max[u][:, r : r + 1], in_=probs[u][:, r, :], axis=AXIS.X, op=ALU.max, negate=True
             )
 
-        def back_mask_and_maximum(u):
-            probs[u] = result.tile([P, ROW_TILES, C_ROWS], F32, name="probs")
-            neg_max[u] = result.tile([P, ROW_TILES], F32, name="neg_max")
-            for r in range(0, ROW_TILES, 2):
-                add_mask(u, r)
-                add_mask(u, r + 1)
-                row_maximum(u, r)
-                row_maximum(u, r + 1)
+        def back_mask_and_maximum(u, r):
+            if r == 0:
+                start_back(u)
+            add_mask(u, r)
+            add_mask(u, r + 1)
+            row_maximum(u, r)
+            row_maximum(u, r + 1)
 
-        def back_exp(u):
-            row_sum[u] = result.tile([P, ROW_TILES], F32, name="row_sum")
-            for r in range(ROW_TILES):
+        def back_exp(u, tiles=range(ROW_TILES)):
+            for r in tiles:
+                if r == 0:
+                    row_sum[u] = result.tile([P, ROW_TILES], F32, name="row_sum")
                 nc.scalar.activation(
                     out=probs[u][:, r, :],
                     in_=probs[u][:, r, :],
@@ -316,66 +336,178 @@ def tile_attention_pa_t_kernel(
                     accum_out=row_sum[u][:, r : r + 1],
                 )
 
-        def back_reciprocal(u):
-            inv_sum[u] = result.tile([P, ROW_TILES], F32, name="inv_sum")
-            nc.vector.reciprocal(out=inv_sum[u][:], in_=row_sum[u][:])
+        def back_reciprocal(u, first=0, last=ROW_TILES):
+            if first == 0:
+                inv_sum[u] = result.tile([P, ROW_TILES], F32, name="inv_sum")
+            nc.vector.reciprocal(out=inv_sum[u][:, first:last], in_=row_sum[u][:, first:last])
 
-        def back_divide_and_store(u):
-            engine = nc.vector if u >= UNITS - 2 else nc.gpsimd
+        def divide(engine, u, r):
+            probabilities = probs[u][:, r, :]
+            factor = inv_sum[u][:, r : r + 1]
+            engine.tensor_scalar(
+                out=probabilities, in0=probabilities, scalar1=factor, scalar2=0.0, op0=ALU.mult, op1=ALU.add
+            )
+
+        def divide_on_scalar(u, r):
+            probabilities = probs[u][:, r, :]
+            nc.scalar.activation(
+                out=probabilities, in_=probabilities, func=ACT.Copy, scale=inv_sum[u][:, r : r + 1]
+            )
+
+        def store(u, r):
             b, h = divmod(u, UNITS_PER_BATCH)
             rows = out[b, h * UNIT_ROWS : (h + 1) * UNIT_ROWS, :].rearrange("(p r) j -> p r j", r=ROW_TILES)
+            nc.sync.dma_start(out=rows[:, r, :], in_=probs[u][:, r, :])
+
+        def back_divide_and_store(u):
             for r in range(ROW_TILES):
-                engine.tensor_scalar(
-                    out=probs[u][:, r, :],
-                    in0=probs[u][:, r, :],
-                    scalar1=inv_sum[u][:, r : r + 1],
-                    scalar2=0.0,
-                    op0=ALU.mult,
-                    op1=ALU.add,
-                )
-                nc.sync.dma_start(out=rows[:, r, :], in_=probs[u][:, r, :])
+                divide(nc.gpsimd, u, r)
+                store(u, r)
 
         def exists(u):
             return 0 <= u < UNITS
 
-        def starts_batch(u):
-            return exists(u) and u % UNITS_PER_BATCH == 0
+        def starts_batch_pair(u):
+            return exists(u) and u % (2 * UNITS_PER_BATCH) == 0
 
-        for step in range(-4, UNITS + 2):
-            if exists(step + 1):
-                mid_regroup_gpsimd(step + 1)
-            if exists(step - 2):
-                back_reciprocal(step - 2)
-                back_divide_and_store(step - 2)
-            if exists(step + 2):
-                mid_matmuls(step + 2, range(0, Q_BANKS))
-            if exists(step):
-                back_matmuls(step, range(SCORE_BANKS, ROW_TILES))
-            if exists(step + 2):
-                mid_matmuls(step + 2, range(Q_BANKS, PACK))
-            if starts_batch(step + 2):
+        order_weight_codes()
+        turn_query_rows(0, 0)
+        copy_query_rows(0, 0)
+        turn_query_rows(0, 1)
+        copy_query_rows(0, 1, on_vector=True)
+        prepare_small_inputs()
+        quantise_query(0)
+        order_weight_scales()
+        spread_context_bits(0)
+        copy_context_bits(0)
+        mid_matmuls(0, range(0, Q_BANKS))
+        mid_bias(0, 0)
+        mid_bias(0, 1)
+        mid_matmuls(0, range(Q_BANKS, PACK))
+        mid_bias(0, 2, on_vector=True)
+        mid_bias(0, 3, on_vector=True)
+        mid_regroup_vector(0, first_row=0)
+        turn_context_rows(0)
+        turn_context_rows(1)
+        copy_context_rows(0)
+        copy_context_rows(1)
+        quantise_context(0)
+        quantise_context(1)
+        turn_query_rows(1, 0)
+        turn_query_rows(1, 1)
+        copy_query_rows(1, 0)
+        copy_query_rows(1, 1)
+        turn_query_rows(2, 0)
+        copy_query_rows(2, 0)
+        mid_quantise(0)
+        back_matmuls(0, range(0, SCORE_BANKS))
+        quantise_query(1)
+        mid_matmuls(1, range(0, Q_BANKS))
+        back_mask_and_maximum(0, 0)
+        back_matmuls(0, range(SCORE_BANKS, ROW_TILES))
+        mid_bias(1, 0)
+        mid_matmuls(1, range(Q_BANKS, PACK))
+        mid_bias(1, 1)
+        mid_bias(1, 2)
+        mid_bias(1, 3)
+        turn_query_rows(2, 1)
+        turn_context_rows(2)
+        copy_query_rows(2, 1)
+        copy_context_rows(2)
+        back_mask_and_maximum(0, 2)
+        front_transposes(3)
+        front_copies(3)
+        quantise_query(2)
+        mid_matmuls(2, range(0, Q_BANKS))
+        mid_regroup_vector(1)
+        mid_regroup_gpsimd(1)
+        mid_quantise(1)
+        back_matmuls(1, range(0, SCORE_BANKS))
+        mid_bias(2, 0)
+        mid_bias(2, 1)
+        mid_bias(2, 2)
+        quantise_context(2)
+        quantise_query(3)
+        quantise_context(3)
+        back_mask_and_maximum(1, 0)
+        back_matmuls(1, range(SCORE_BANKS, ROW_TILES))
+        back_exp(0)
+        mid_matmuls(2, range(Q_BANKS, PACK))
+        mid_bias(2, 3)
+        front_transposes(4)
+        front_copies(4)
+        back_mask_and_maximum(1, 2)
+        mid_regroup_vector(2)
+        mid_regroup_gpsimd(2)
+        mid_matmuls(3, range(0, Q_BANKS))
+        mid_bias(3, 0)
+        mid_matmuls(3, range(Q_BANKS, PACK))
+        mid_bias(3, 1)
+        mid_bias(3, 2)
+        mid_bias(3, 3)
+        mid_quantise(2)
+        back_matmuls(2, range(0, SCORE_BANKS))
+        front_transposes(5)
+        quantise_context(4)
+        quantise_query(4)
+        mid_regroup_vector(3)
+        for step in range(2, last - 1):
+            mid_regroup_gpsimd(step + 1)
+            back_reciprocal(step - 2)
+            back_divide_and_store(step - 2)
+            mid_matmuls(step + 2, range(0, Q_BANKS))
+            back_matmuls(step, range(SCORE_BANKS, ROW_TILES))
+            mid_matmuls(step + 2, range(Q_BANKS, PACK))
+            if starts_batch_pair(step + 2):
                 spread_context_bits((step + 2) // UNITS_PER_BATCH)
             if exists(step + 4):
                 front_transposes(step + 4)
-            if exists(step):
-                back_mask_and_maximum(step)
+            back_mask_and_maximum(step, 0)
+            back_mask_and_maximum(step, 2)
             if exists(step + 3):
                 front_copies(step + 3)
-            if exists(step + 2):
-                mid_bias(step + 2)
-            if starts_batch(step + 2):
+            for t in range(PACK):
+                mid_bias(step + 2, t)
+            if starts_batch_pair(step + 2):
                 copy_context_bits((step + 2) // UNITS_PER_BATCH)
-            if exists(step):
-                back_exp(step)
-            if exists(step + 1):
-                mid_quantise(step + 1)
-                back_matmuls(step + 1, range(0, SCORE_BANKS))
-            if step + 3 == 0:
-                order_weights()
+            back_exp(step - 1)
+            mid_quantise(step + 1)
+            back_matmuls(step + 1, range(0, SCORE_BANKS))
             if exists(step + 3):
-                quantise_query(step + 3)
                 quantise_context(step + 3)
-            if step + 1 == 0:
-                prepare_mask_weight()
-            if exists(step + 2):
+                quantise_query(step + 3)
+            if step + 2 < last:
                 mid_regroup_vector(step + 2)
+        mid_regroup_gpsimd(last)
+        back_reciprocal(last - 3)
+        back_divide_and_store(last - 3)
+        back_matmuls(last - 1, range(SCORE_BANKS, ROW_TILES))
+        back_exp(last - 2)
+        back_mask_and_maximum(last - 1, 0)
+        mid_quantise(last)
+        back_reciprocal(last - 2)
+        back_divide_and_store(last - 2)
+        back_mask_and_maximum(last - 1, 2)
+        back_matmuls(last, range(0, SCORE_BANKS))
+        back_exp(last - 1)
+        start_back(last)
+        add_mask(last, 0)
+        add_mask(last, 1)
+        back_matmuls(last, range(SCORE_BANKS, ROW_TILES))
+        back_reciprocal(last - 1)
+        for r in (2, 3):
+            divide_on_scalar(last - 1, r)
+            store(last - 1, r)
+        for r in (0, 1):
+            divide(nc.gpsimd, last - 1, r)
+            store(last - 1, r)
+        row_maximum(last, 0)
+        row_maximum(last, 1)
+        back_mask_and_maximum(last, 2)
+        back_exp(last)
+        back_reciprocal(last, 0, 3)
+        for r in range(ROW_TILES):
+            if r == 2:
+                back_reciprocal(last, 3, 4)
+            divide(nc.vector, last, r)
+            store(last, r)

@@ -22,7 +22,7 @@ UNITS_PER_BATCH = Q_ROWS // UNIT_ROWS
 UNITS = BATCHES * UNITS_PER_BATCH
 PIECE_ROWS = C_ROWS // UNITS_PER_BATCH
 PIECE_TILES = PIECE_ROWS // P
-GPSIMD_ROWS = 384
+GPSIMD_ROWS = 256
 MASK_PENALTY = 10000.0
 TURN_BANKS, Q_BANKS, SCORE_BANKS = 3, 3, 2
 

@@ -59,14 +59,12 @@ def tile_attention_pa_t_kernel(
             rows = context[b, h * PIECE_ROWS : (h + 1) * PIECE_ROWS, :]
             nc.sync.dma_start(out=c_raw[u][:], in_=rows.rearrange("(r p) d -> p r d", p=P))
 
-        w_scales_raw = const.tile([P, FEATURES], U8, name="w_scales_raw", align_bytes=64)
-        nc.vector.memset(w_scales_raw[:].bitcast(I32), 0)
-        for quadrant in range(4):
-            nc.sync.dma_start(
-                out=w_scales_raw[32 * quadrant : 32 * quadrant + 4, :].bitcast(I32),
-                in_=W_in_scales[0, 4 * quadrant : 4 * quadrant + 4, :].bitcast(I32),
-            )
         load_query_rows(0, pieces=2)
+
+        cbit_raw = const.tile([BATCHES, C_ROWS], BF16, name="cbit_raw")
+        nc.sync.dma_start(out=cbit_raw[:], in_=context_bit)
+        cbit_rows = const.tile([P, C_ROWS], BF16, name="cbit_rows")
+        nc.vector.memset(cbit_rows[:], 0.0)
 
         w_words_raw = const.tile([P, FEATURES], U32, name="w_words_raw", align_bytes=64)
         nc.sync.dma_start(
@@ -74,20 +72,23 @@ def tile_attention_pa_t_kernel(
             in_=W_in_words.rearrange("g p n t -> (g p) (n t)").bitcast(I32),
         )
 
-        row_inputs = const.tile([P, UNIT_ROWS], BF16, name="row_inputs")
-        nc.vector.memset(row_inputs[:], 0.0)
-        nc.sync.dma_start(
-            out=row_inputs[0:UNITS, :], in_=query_bit.rearrange("b (h i) -> (b h) i", i=UNIT_ROWS)
-        )
-        nc.sync.dma_start(out=row_inputs[UNITS : UNITS + 1, :], in_=b_in.rearrange("(o n) -> o n", o=1))
+        bias_row = const.tile([P, FEATURES], BF16, name="bias_row")
+        nc.vector.memset(bias_row[:], 0.0)
+        nc.sync.dma_start(out=bias_row[0:1, :], in_=b_in.rearrange("(o n) -> o n", o=1))
 
-        cbit_raw = const.tile([BATCHES, C_ROWS], BF16, name="cbit_raw")
-        nc.sync.dma_start(out=cbit_raw[:], in_=context_bit)
-        cbit_rows = const.tile([P, C_ROWS], BF16, name="cbit_rows")
-        nc.vector.memset(cbit_rows[:], 0.0)
-
+        w_scales_raw = const.tile([P, FEATURES], U8, name="w_scales_raw", align_bytes=64)
+        nc.vector.memset(w_scales_raw[:].bitcast(I32), 0)
+        for quadrant in range(4):
+            nc.sync.dma_start(
+                out=w_scales_raw[32 * quadrant : 32 * quadrant + 4, :].bitcast(I32),
+                in_=W_in_scales[0, 4 * quadrant : 4 * quadrant + 4, :].bitcast(I32),
+            )
         for u in range(UNITS_PER_BATCH):
             load_context_rows(u)
+
+        qbit_rows = const.tile([P, UNIT_ROWS], BF16, name="qbit_rows")
+        nc.vector.memset(qbit_rows[:], 0.0)
+        nc.sync.dma_start(out=qbit_rows[0:UNITS, :], in_=query_bit.rearrange("b (h i) -> (b h) i", i=UNIT_ROWS))
 
         load_query_rows(1)
         for u in range(2, UNITS):
@@ -118,22 +119,31 @@ def tile_attention_pa_t_kernel(
                 in_=w_scales_raw[:].rearrange("p (m t) -> p m t", t=PACK),
             )
 
-        def prepare_small_inputs():
-            turned = turn_banks.tile([P, ROW_TILES, P], BF16, name="rows_turned", tag="turned")
-            for r in range(ROW_TILES):
+        def turn_every_fourth(rows, name):
+            turned = turn_banks.tile([P, PACK, P], BF16, name=name, tag="turned")
+            for t in range(PACK):
                 nc.tensor.transpose(
-                    out=turned[:, r, :], in_=row_inputs[:, r:UNIT_ROWS:ROW_TILES], identity=ident_bf16[:]
+                    out=turned[:, t, :], in_=rows[:, t : PACK * P : PACK], identity=ident_bf16[:]
                 )
-            nc.vector.tensor_copy(out=bias_cols[:], in_=turned[:, :, UNITS])
+            return turned
+
+        def prepare_bias():
+            turned = turn_every_fourth(bias_row, "bias_turned")
+            nc.vector.tensor_copy(out=bias_cols[:], in_=turned[:, :, 0])
+
+        def prepare_mask_weight():
+            turned = turn_every_fourth(qbit_rows, "qbit_turned")
             nc.vector.tensor_scalar_mul(
                 out=mask_weight[:], in0=turned[:, :, 0:UNITS], scalar1=MASK_PENALTY
             )
+
+        def prepare_context_bits():
             nc.vector.tensor_scalar_add(out=cbit_rows[0:BATCHES, :], in0=cbit_raw[:], scalar1=-1.0)
 
         cbit_spread = {}
 
         def spread_context_bits(b):
-            cbit_spread[b] = q_banks.tile([P, 2, C_ROWS], BF16, name="cbit_spread", tag="q_sums")
+            cbit_spread[b] = score_banks.tile([P, 2, C_ROWS], BF16, name="cbit_spread", tag="score_sums")
             for i in range(2):
                 nc.tensor.matmul(
                     out=cbit_spread[b][:, i, :],
@@ -367,32 +377,33 @@ def tile_attention_pa_t_kernel(
         def exists(u):
             return 0 <= u < UNITS
 
-        def starts_batch_pair(u):
-            return exists(u) and u % (2 * UNITS_PER_BATCH) == 0
-
+        prepare_context_bits()
         order_weight_codes()
         turn_query_rows(0, 0)
         copy_query_rows(0, 0)
         turn_query_rows(0, 1)
         copy_query_rows(0, 1, on_vector=True)
-        prepare_small_inputs()
-        quantise_query(0)
-        order_weight_scales()
         spread_context_bits(0)
         copy_context_bits(0)
+        prepare_bias()
+        spread_context_bits(2)
+        quantise_query(0)
+        order_weight_scales()
         mid_matmuls(0, range(0, Q_BANKS))
         mid_bias(0, 0)
         mid_bias(0, 1)
-        mid_matmuls(0, range(Q_BANKS, PACK))
+        copy_context_bits(2)
         mid_bias(0, 2, on_vector=True)
+        prepare_mask_weight()
+        mid_matmuls(0, range(Q_BANKS, PACK))
         mid_bias(0, 3, on_vector=True)
         mid_regroup_vector(0, first_row=0)
+        spread_context_bits(4)
         turn_context_rows(0)
         turn_context_rows(1)
+        copy_context_bits(4)
         copy_context_rows(0)
         copy_context_rows(1)
-        quantise_context(0)
-        quantise_context(1)
         turn_query_rows(1, 0)
         turn_query_rows(1, 1)
         copy_query_rows(1, 0)
@@ -400,6 +411,8 @@ def tile_attention_pa_t_kernel(
         turn_query_rows(2, 0)
         copy_query_rows(2, 0)
         mid_quantise(0)
+        quantise_context(0)
+        quantise_context(1)
         back_matmuls(0, range(0, SCORE_BANKS))
         quantise_query(1)
         mid_matmuls(1, range(0, Q_BANKS))
@@ -458,8 +471,8 @@ def tile_attention_pa_t_kernel(
             mid_matmuls(step + 2, range(0, Q_BANKS))
             back_matmuls(step, range(SCORE_BANKS, ROW_TILES))
             mid_matmuls(step + 2, range(Q_BANKS, PACK))
-            if starts_batch_pair(step + 2):
-                spread_context_bits((step + 2) // UNITS_PER_BATCH)
+            if step + 2 == 6 * UNITS_PER_BATCH:
+                spread_context_bits(6)
             if exists(step + 4):
                 front_transposes(step + 4)
             back_mask_and_maximum(step, 0)
@@ -468,8 +481,8 @@ def tile_attention_pa_t_kernel(
                 front_copies(step + 3)
             for t in range(PACK):
                 mid_bias(step + 2, t)
-            if starts_batch_pair(step + 2):
-                copy_context_bits((step + 2) // UNITS_PER_BATCH)
+            if step + 2 == 6 * UNITS_PER_BATCH:
+                copy_context_bits(6)
             back_exp(step - 1)
             mid_quantise(step + 1)
             back_matmuls(step + 1, range(0, SCORE_BANKS))

@@ -22,7 +22,8 @@ UNITS_PER_BATCH = Q_ROWS // UNIT_ROWS
 UNITS = BATCHES * UNITS_PER_BATCH
 PIECE_ROWS = C_ROWS // UNITS_PER_BATCH
 PIECE_TILES = PIECE_ROWS // P
-GPSIMD_ROWS = 256
+GPSIMD_TILES = 3
+PLANE_ROWS = 384
 MASK_PENALTY = 10000.0
 TURN_BANKS, Q_BANKS, SCORE_BANKS = 3, 3, 2
 
@@ -160,7 +161,7 @@ def tile_attention_pa_t_kernel(
 
         x_turned, c_turned, x_grouped, c_grouped = {}, {}, {}, {}
         x_words, x_scales, c_words, c_scales = {}, {}, {}, {}
-        q_sums, q_planes, q_grouped, q_words, q_scales = {}, {}, {}, {}, {}
+        q_sums, joint_sums, q_planes, q_grouped, q_words, q_scales = {}, {}, {}, {}, {}, {}
         score_sums, probs, neg_max, row_sum, inv_sum = {}, {}, {}, {}, {}
 
         def turn_query_rows(u, pair):
@@ -234,23 +235,34 @@ def tile_attention_pa_t_kernel(
                 in_=c_grouped[u][:].rearrange("p j t -> p (j t)"),
             )
 
+        def mid_pass(out, t, u, first_row, last_row):
+            rows = slice(first_row, last_row)
+            nc.tensor.matmul_mx(
+                out=out,
+                lhsT=w_words[:, t * P : (t + 1) * P].bitcast(FP8X4),
+                lhsT_scale=w_scales[:, t * P : (t + 1) * P],
+                rhs=x_words[u][:, rows].bitcast(FP8X4),
+                rhs_scale=x_scales[u][:, rows],
+                start=True,
+                stop=True,
+            )
+
         def mid_matmuls(u, planes):
             for t in planes:
-                sums = q_banks.tile([P, UNIT_ROWS], F32, name="q_sums")
+                sums = q_banks.tile([P, PLANE_ROWS], F32, name="q_sums")
                 q_sums[u, t] = sums
-                nc.tensor.matmul_mx(
-                    out=sums[:],
-                    lhsT=w_words[:, t * P : (t + 1) * P].bitcast(FP8X4),
-                    lhsT_scale=w_scales[:, t * P : (t + 1) * P],
-                    rhs=x_words[u][:].bitcast(FP8X4),
-                    rhs_scale=x_scales[u][:],
-                    start=True,
-                    stop=True,
-                )
+                mid_pass(sums[:, 0:256], t, u, 0, 256)
+                mid_pass(sums[:, 256:PLANE_ROWS], t, u, 256, PLANE_ROWS)
+
+        def mid_matmuls_joint(u):
+            sums = q_banks.tile([P, PACK, P], F32, name="joint_sums", tag="q_sums")
+            joint_sums[u] = sums
+            for t in range(PACK):
+                mid_pass(sums[:, t, :], t, u, PLANE_ROWS, UNIT_ROWS)
 
         def mid_bias(u, t, on_vector=False):
             if t == 0:
-                q_planes[u] = work.tile([P, PACK, UNIT_ROWS], BF16, name="q_planes")
+                q_planes[u] = work.tile([P, PACK, PLANE_ROWS], BF16, name="q_planes")
             bias = bias_cols[:, t : t + 1]
             if on_vector:
                 nc.vector.tensor_scalar_add(out=q_planes[u][:, t, :], in0=q_sums[u, t][:], scalar1=bias)
@@ -259,23 +271,29 @@ def tile_attention_pa_t_kernel(
                     out=q_planes[u][:, t, :], in_=q_sums[u, t][:], func=ACT.Identity, bias=bias, scale=1.0
                 )
 
+        def mid_bias_joint(u):
+            nc.vector.tensor_tensor(
+                out=grouped_tile(u)[:, PLANE_ROWS:, :],
+                in0=joint_sums[u][:].rearrange("p t c -> p c t"),
+                in1=bias_cols[:].unsqueeze(1).to_broadcast([P, P, PACK]),
+                op=ALU.add,
+            )
+
         def grouped_tile(u):
             if u not in q_grouped:
                 q_grouped[u] = work.tile([P, UNIT_ROWS, PACK], BF16, name="q_grouped", align_bytes=64)
             return q_grouped[u]
 
-        def mid_regroup_vector(u, first_row=GPSIMD_ROWS):
-            grouped = grouped_tile(u)
+        def mid_regroup_vector(u):
             nc.vector.tensor_copy(
-                out=grouped[:, first_row:, :].rearrange("p (c i) t -> p c t i", i=4),
-                in_=q_planes[u][:, :, first_row:].rearrange("p t (c i) -> p c t i", i=4),
+                out=grouped_tile(u)[:, 0:PLANE_ROWS, :].rearrange("p (c i) t -> p c t i", i=4),
+                in_=q_planes[u][:].rearrange("p t (c i) -> p c t i", i=4),
             )
 
         def mid_regroup_gpsimd(u):
-            rows = UNIT_ROWS if u == last else GPSIMD_ROWS
             nc.gpsimd.tensor_scalar(
-                out=grouped_tile(u)[:, 0:rows, :],
-                in0=q_planes[u][:, :, 0:rows].rearrange("p t c -> p c t"),
+                out=grouped_tile(u)[:, 0:PLANE_ROWS, :],
+                in0=q_planes[u][:].rearrange("p t c -> p c t"),
                 scalar1=1.0,
                 scalar2=0.0,
                 op0=ALU.mult,
@@ -369,9 +387,14 @@ def tile_attention_pa_t_kernel(
             rows = out[b, h * UNIT_ROWS : (h + 1) * UNIT_ROWS, :].rearrange("(p r) j -> p r j", r=ROW_TILES)
             nc.sync.dma_start(out=rows[:, r, :], in_=probs[u][:, r, :])
 
-        def back_divide_and_store(u):
-            for r in range(ROW_TILES):
+        def back_divide_and_store(u, on_gpsimd):
+            for r in range(on_gpsimd):
                 divide(nc.gpsimd, u, r)
+                store(u, r)
+
+        def back_divide_and_store_rest(u, on_gpsimd):
+            for r in range(on_gpsimd, ROW_TILES):
+                divide_on_scalar(u, r)
                 store(u, r)
 
         def exists(u):
@@ -396,8 +419,10 @@ def tile_attention_pa_t_kernel(
         mid_bias(0, 2, on_vector=True)
         prepare_mask_weight()
         mid_matmuls(0, range(Q_BANKS, PACK))
+        mid_matmuls_joint(0)
         mid_bias(0, 3, on_vector=True)
-        mid_regroup_vector(0, first_row=0)
+        mid_bias_joint(0)
+        mid_regroup_vector(0)
         spread_context_bits(4)
         turn_context_rows(0)
         turn_context_rows(1)
@@ -420,6 +445,7 @@ def tile_attention_pa_t_kernel(
         back_matmuls(0, range(SCORE_BANKS, ROW_TILES))
         mid_bias(1, 0)
         mid_matmuls(1, range(Q_BANKS, PACK))
+        mid_matmuls_joint(1)
         mid_bias(1, 1)
         mid_bias(1, 2)
         mid_bias(1, 3)
@@ -432,7 +458,7 @@ def tile_attention_pa_t_kernel(
         front_copies(3)
         quantise_query(2)
         mid_matmuls(2, range(0, Q_BANKS))
-        mid_regroup_vector(1)
+        mid_bias_joint(1)
         mid_regroup_gpsimd(1)
         mid_quantise(1)
         back_matmuls(1, range(0, SCORE_BANKS))
@@ -446,15 +472,17 @@ def tile_attention_pa_t_kernel(
         back_matmuls(1, range(SCORE_BANKS, ROW_TILES))
         back_exp(0)
         mid_matmuls(2, range(Q_BANKS, PACK))
+        mid_matmuls_joint(2)
         mid_bias(2, 3)
         front_transposes(4)
         front_copies(4)
         back_mask_and_maximum(1, 2)
-        mid_regroup_vector(2)
+        mid_bias_joint(2)
         mid_regroup_gpsimd(2)
         mid_matmuls(3, range(0, Q_BANKS))
         mid_bias(3, 0)
         mid_matmuls(3, range(Q_BANKS, PACK))
+        mid_matmuls_joint(3)
         mid_bias(3, 1)
         mid_bias(3, 2)
         mid_bias(3, 3)
@@ -463,14 +491,15 @@ def tile_attention_pa_t_kernel(
         front_transposes(5)
         quantise_context(4)
         quantise_query(4)
-        mid_regroup_vector(3)
+        back_reciprocal(0)
+        mid_bias_joint(3)
         for step in range(2, last - 1):
+            back_divide_and_store(step - 2, GPSIMD_TILES)
             mid_regroup_gpsimd(step + 1)
-            back_reciprocal(step - 2)
-            back_divide_and_store(step - 2)
             mid_matmuls(step + 2, range(0, Q_BANKS))
             back_matmuls(step, range(SCORE_BANKS, ROW_TILES))
             mid_matmuls(step + 2, range(Q_BANKS, PACK))
+            mid_matmuls_joint(step + 2)
             if step + 2 == 6 * UNITS_PER_BATCH:
                 spread_context_bits(6)
             if exists(step + 4):
@@ -484,40 +513,43 @@ def tile_attention_pa_t_kernel(
             if step + 2 == 6 * UNITS_PER_BATCH:
                 copy_context_bits(6)
             back_exp(step - 1)
+            back_divide_and_store_rest(step - 2, GPSIMD_TILES)
             mid_quantise(step + 1)
             back_matmuls(step + 1, range(0, SCORE_BANKS))
             if exists(step + 3):
                 quantise_context(step + 3)
                 quantise_query(step + 3)
-            if step + 2 < last:
-                mid_regroup_vector(step + 2)
+            back_reciprocal(step - 1)
+            mid_bias_joint(step + 2)
+        back_divide_and_store(last - 3, 2)
         mid_regroup_gpsimd(last)
-        back_reciprocal(last - 3)
-        back_divide_and_store(last - 3)
         back_matmuls(last - 1, range(SCORE_BANKS, ROW_TILES))
         back_exp(last - 2)
+        back_divide_and_store_rest(last - 3, 2)
         back_mask_and_maximum(last - 1, 0)
+        add_mask(last - 1, 2)
+        add_mask(last - 1, 3)
         mid_quantise(last)
-        back_reciprocal(last - 2)
-        back_divide_and_store(last - 2)
-        back_mask_and_maximum(last - 1, 2)
         back_matmuls(last, range(0, SCORE_BANKS))
+        row_maximum(last - 1, 2)
+        row_maximum(last - 1, 3)
         back_exp(last - 1)
+        back_reciprocal(last - 2)
+        back_divide_and_store(last - 2, 2)
+        back_divide_and_store_rest(last - 2, 2)
         start_back(last)
         add_mask(last, 0)
         add_mask(last, 1)
         back_matmuls(last, range(SCORE_BANKS, ROW_TILES))
-        back_reciprocal(last - 1)
-        for r in (2, 3):
-            divide_on_scalar(last - 1, r)
-            store(last - 1, r)
-        for r in (0, 1):
-            divide(nc.gpsimd, last - 1, r)
-            store(last - 1, r)
         row_maximum(last, 0)
         row_maximum(last, 1)
+        back_reciprocal(last - 1)
+        back_divide_and_store(last - 1, 2)
         back_mask_and_maximum(last, 2)
         back_exp(last)
+        for r in range(2, ROW_TILES):
+            divide(nc.vector, last - 1, r)
+            store(last - 1, r)
         back_reciprocal(last, 0, 3)
         for r in range(ROW_TILES):
             if r == 2:

@@ -397,9 +397,15 @@ def tile_attention_pa_t_kernel(
                 divide_on_scalar(u, r)
                 store(u, r)
 
+        def keep_warm(passes):
+            idle = score_banks.tile([P, C_ROWS], F32, name="idle", tag="score_sums")
+            for i in range(passes):
+                nc.tensor.matmul(out=idle[:], lhsT=cbit_rows[:, 0:P], rhs=cbit_rows[:], start=True, stop=True)
+
         def exists(u):
             return 0 <= u < UNITS
 
+        keep_warm(5)
         prepare_context_bits()
         order_weight_codes()
         turn_query_rows(0, 0)
@@ -541,15 +547,17 @@ def tile_attention_pa_t_kernel(
         add_mask(last, 0)
         add_mask(last, 1)
         back_matmuls(last, range(SCORE_BANKS, ROW_TILES))
+        back_reciprocal(last - 1)
         row_maximum(last, 0)
         row_maximum(last, 1)
-        back_reciprocal(last - 1)
+        back_exp(last, [0, 1])
         back_divide_and_store(last - 1, 2)
+        divide_on_scalar(last - 1, 2)
+        store(last - 1, 2)
         back_mask_and_maximum(last, 2)
-        back_exp(last)
-        for r in range(2, ROW_TILES):
-            divide(nc.vector, last - 1, r)
-            store(last - 1, r)
+        divide(nc.vector, last - 1, 3)
+        store(last - 1, 3)
+        back_exp(last, [2, 3])
         back_reciprocal(last, 0, 3)
         for r in range(ROW_TILES):
             if r == 2:

@@ -143,8 +143,8 @@ def tile_attention_pa_t_kernel(
 
         cbit_spread = {}
 
-        def spread_context_bits(b):
-            cbit_spread[b] = score_banks.tile([P, 2, C_ROWS], BF16, name="cbit_spread", tag="score_sums")
+        def spread_context_bits(b, banks=score_banks, tag="score_sums"):
+            cbit_spread[b] = banks.tile([P, 2, C_ROWS], BF16, name="cbit_spread", tag=tag)
             for i in range(2):
                 nc.tensor.matmul(
                     out=cbit_spread[b][:, i, :],
@@ -439,8 +439,10 @@ def tile_attention_pa_t_kernel(
         turn_query_rows(1, 1)
         copy_query_rows(1, 0)
         copy_query_rows(1, 1)
+        spread_context_bits(6, q_banks, "q_sums")
         turn_query_rows(2, 0)
         copy_query_rows(2, 0)
+        copy_context_bits(6)
         mid_quantise(0)
         quantise_context(0)
         quantise_context(1)
@@ -506,8 +508,6 @@ def tile_attention_pa_t_kernel(
             back_matmuls(step, range(SCORE_BANKS, ROW_TILES))
             mid_matmuls(step + 2, range(Q_BANKS, PACK))
             mid_matmuls_joint(step + 2)
-            if step + 2 == 6 * UNITS_PER_BATCH:
-                spread_context_bits(6)
             if exists(step + 4):
                 front_transposes(step + 4)
             back_mask_and_maximum(step, 0)
@@ -516,8 +516,6 @@ def tile_attention_pa_t_kernel(
                 front_copies(step + 3)
             for t in range(PACK):
                 mid_bias(step + 2, t)
-            if step + 2 == 6 * UNITS_PER_BATCH:
-                copy_context_bits(6)
             back_exp(step - 1)
             back_divide_and_store_rest(step - 2, GPSIMD_TILES)
             mid_quantise(step + 1)

from contextlib import ExitStack

import concourse.mybir as mybir
from concourse.masks import make_identity

F32 = mybir.dt.float32
BF16 = mybir.dt.bfloat16
I32 = mybir.dt.int32
U32 = mybir.dt.uint32
U8 = mybir.dt.uint8
FP8X4 = mybir.dt.float8_e4m3fn_x4
ALU = mybir.AluOpType
ACT = mybir.ActivationFunctionType
AXIS = mybir.AxisListType

P = 128
PACK = 4
BATCHES, Q_ROWS, C_ROWS, FEATURES = 8, 1024, 512, 512
UNIT_ROWS = 512
ROW_TILES = UNIT_ROWS // P
UNITS_PER_BATCH = Q_ROWS // UNIT_ROWS
UNITS = BATCHES * UNITS_PER_BATCH
PIECE_ROWS = C_ROWS // UNITS_PER_BATCH
PIECE_TILES = PIECE_ROWS // P
GPSIMD_TILES = 3
PLANE_ROWS = 384
MASK_PENALTY = 10000.0
TURN_BANKS, Q_BANKS, SCORE_BANKS = 3, 3, 2

FLOPS = 2 * BATCHES * Q_ROWS * FEATURES * FEATURES + 2 * BATCHES * Q_ROWS * C_ROWS * FEATURES


def tile_attention_pa_t_kernel(
    tc, query, context, query_bit, context_bit, W_in_words, W_in_scales, b_in, out
):
    nc = tc.nc
    with ExitStack() as stack:
        stack.enter_context(tc.manual_schedule())
        const = stack.enter_context(tc.tile_pool(name="const", bufs=1))
        work = stack.enter_context(tc.tile_pool(name="work", bufs=2))
        result = stack.enter_context(tc.tile_pool(name="result", bufs=5))
        turn_banks = stack.enter_context(tc.psum_pool(name="turn_banks", bufs=TURN_BANKS))
        q_banks = stack.enter_context(tc.psum_pool(name="q_banks", bufs=Q_BANKS))
        score_banks = stack.enter_context(tc.psum_pool(name="score_banks", bufs=SCORE_BANKS))

        x_raw = {}
        c_raw = {}

        def load_query_rows(u, pieces=1):
            b, h = divmod(u, UNITS_PER_BATCH)
            x_raw[u] = const.tile([P, ROW_TILES, FEATURES], BF16, name="x_raw%d" % u)
            rows = query[b, h * UNIT_ROWS : (h + 1) * UNIT_ROWS, :].rearrange("(p r) k -> p r k", r=ROW_TILES)
            step = ROW_TILES // pieces
            for r in range(0, ROW_TILES, step):
                nc.sync.dma_start(out=x_raw[u][:, r : r + step, :], in_=rows[:, r : r + step, :])

        def load_context_rows(u):
            b, h = divmod(u, UNITS_PER_BATCH)
            c_raw[u] = const.tile([P, PIECE_TILES, FEATURES], BF16, name="c_raw%d" % u)
            rows = context[b, h * PIECE_ROWS : (h + 1) * PIECE_ROWS, :]
            nc.sync.dma_start(out=c_raw[u][:], in_=rows.rearrange("(r p) d -> p r d", p=P))

        load_query_rows(0, pieces=2)

        cbit_raw = const.tile([BATCHES, C_ROWS], BF16, name="cbit_raw")
        nc.sync.dma_start(out=cbit_raw[:], in_=context_bit)
        cbit_rows = const.tile([P, C_ROWS], BF16, name="cbit_rows")
        nc.vector.memset(cbit_rows[:], 0.0)

        w_words_raw = const.tile([P, FEATURES], U32, name="w_words_raw", align_bytes=64)
        nc.sync.dma_start(
            out=w_words_raw[:].bitcast(I32),
            in_=W_in_words.rearrange("g p n t -> (g p) (n t)").bitcast(I32),
        )

        bias_row = const.tile([P, FEATURES], BF16, name="bias_row")
        nc.vector.memset(bias_row[:], 0.0)
        nc.sync.dma_start(out=bias_row[0:1, :], in_=b_in.rearrange("(o n) -> o n", o=1))

        w_scales_raw = const.tile([P, FEATURES], U8, name="w_scales_raw", align_bytes=64)
        nc.vector.memset(w_scales_raw[:].bitcast(I32), 0)
        for quadrant in range(4):
            nc.sync.dma_start(
                out=w_scales_raw[32 * quadrant : 32 * quadrant + 4, :].bitcast(I32),
                in_=W_in_scales[0, 4 * quadrant : 4 * quadrant + 4, :].bitcast(I32),
            )
        for u in range(UNITS_PER_BATCH):
            load_context_rows(u)

        qbit_rows = const.tile([P, UNIT_ROWS], BF16, name="qbit_rows")
        nc.vector.memset(qbit_rows[:], 0.0)
        nc.sync.dma_start(out=qbit_rows[0:UNITS, :], in_=query_bit.rearrange("b (h i) -> (b h) i", i=UNIT_ROWS))

        load_query_rows(1)
        for u in range(2, UNITS):
            load_query_rows(u)
            load_context_rows(u)

        ident_f32 = const.tile([P, P], F32, name="ident_f32")
        make_identity(nc, ident_f32[:])
        ident_bf16 = const.tile([P, P], BF16, name="ident_bf16")
        make_identity(nc, ident_bf16[:])

        mask_weight = const.tile([P, ROW_TILES, UNITS], F32, name="mask_weight")
        bias_cols = const.tile([P, PACK], F32, name="bias_cols")
        cbit_minus_1 = const.tile([P, BATCHES, C_ROWS], BF16, name="cbit_minus_1")

        w_words = const.tile([P, FEATURES], U32, name="w_words", align_bytes=64)
        w_scales = const.tile([P, FEATURES], U8, name="w_scales", align_bytes=64)

        def order_weight_codes():
            nc.vector.tensor_copy(
                out=w_words[:].bitcast(I32).rearrange("p (t m) -> p m t", t=PACK),
                in_=w_words_raw[:].bitcast(I32).rearrange("p (m t) -> p m t", t=PACK),
            )

        def order_weight_scales():
            nc.vector.tensor_copy(
                out=w_scales[:].rearrange("p (t m) -> p m t", t=PACK),
                in_=w_scales_raw[:].rearrange("p (m t) -> p m t", t=PACK),
            )

        def turn_every_fourth(rows, name):
            turned = turn_banks.tile([P, PACK, P], BF16, name=name, tag="turned")
            for t in range(PACK):
                nc.tensor.transpose(
                    out=turned[:, t, :], in_=rows[:, t : PACK * P : PACK], identity=ident_bf16[:]
                )
            return turned

        def prepare_bias():
            turned = turn_every_fourth(bias_row, "bias_turned")
            nc.vector.tensor_copy(out=bias_cols[:], in_=turned[:, :, 0])

        def prepare_mask_weight():
            turned = turn_every_fourth(qbit_rows, "qbit_turned")
            nc.vector.tensor_scalar_mul(
                out=mask_weight[:], in0=turned[:, :, 0:UNITS], scalar1=MASK_PENALTY
            )

        def prepare_context_bits():
            nc.vector.tensor_scalar_add(out=cbit_rows[0:BATCHES, :], in0=cbit_raw[:], scalar1=-1.0)

        cbit_spread = {}

        def spread_context_bits(b, banks=score_banks, tag="score_sums"):
            cbit_spread[b] = banks.tile([P, 2, C_ROWS], BF16, name="cbit_spread", tag=tag)
            for i in range(2):
                nc.tensor.matmul(
                    out=cbit_spread[b][:, i, :],
                    lhsT=ident_bf16[:, b + i : b + i + 1].to_broadcast([P, P]),
                    rhs=cbit_rows[:],
                    start=True,
                    stop=True,
                )

        def copy_context_bits(b):
            nc.scalar.copy(out=cbit_minus_1[:, b : b + 2, :], in_=cbit_spread[b][:])

        last = UNITS - 1

        x_turned, c_turned, x_grouped, c_grouped = {}, {}, {}, {}
        x_words, x_scales, c_words, c_scales = {}, {}, {}, {}
        q_sums, joint_sums, q_planes, q_grouped, q_words, q_scales = {}, {}, {}, {}, {}, {}
        score_sums, probs, neg_max, row_sum, inv_sum = {}, {}, {}, {}, {}

        def turn_query_rows(u, pair):
            turned = turn_banks.tile([P, 2, 2, P], F32, name="x_turned", tag="turned")
            x_turned[u, pair] = turned
            for rr in range(2):
                words = x_raw[u][:, 2 * pair + rr, :].bitcast(F32)
                for half in range(2):
                    nc.tensor.transpose(
                        out=turned[:, rr, half, :],
                        in_=words[:, half : FEATURES // 2 : 2],
                        identity=ident_f32[:],
                    )

        def turn_context_rows(u):
            turned = turn_banks.tile([P, PIECE_TILES, 2, P], F32, name="c_turned", tag="turned")
            c_turned[u] = turned
            for rr in range(PIECE_TILES):
                words = c_raw[u][:, rr, :].bitcast(F32)
                for half in range(2):
                    nc.tensor.transpose(
                        out=turned[:, rr, half, :],
                        in_=words[:, half : FEATURES // 2 : 2],
                        identity=ident_f32[:],
                    )

        def front_transposes(u):
            turn_query_rows(u, 0)
            turn_query_rows(u, 1)
            turn_context_rows(u)

        def copy_query_rows(u, pair, on_vector=False):
            if pair == 0:
                x_grouped[u] = work.tile([P, UNIT_ROWS, PACK], BF16, name="x_grouped", align_bytes=64)
            copy = nc.vector.tensor_copy if on_vector else nc.scalar.copy
            as_words = x_grouped[u][:].rearrange("p c t -> p (c t)").bitcast(F32)
            as_words = as_words.rearrange("p (pair r i half) -> p pair r i half", r=2, i=P, half=2)
            copy(out=as_words[:, pair], in_=x_turned[u, pair][:].rearrange("p r half i -> p r i half"))

        def copy_context_rows(u):
            c_grouped[u] = work.tile([P, PIECE_ROWS, PACK], BF16, name="c_grouped", align_bytes=64)
            as_words = c_grouped[u][:].rearrange("p j t -> p (j t)").bitcast(F32)
            nc.scalar.copy(
                out=as_words.rearrange("p (r j half) -> p r j half", j=P, half=2),
                in_=c_turned[u][:].rearrange("p r half j -> p r j half"),
            )

        def front_copies(u):
            copy_query_rows(u, 0)
            copy_query_rows(u, 1)
            copy_context_rows(u)

        def quantise_query(u):
            x_words[u] = work.tile([P, UNIT_ROWS], U32, name="x_words", align_bytes=64)
            x_scales[u] = work.tile([P, UNIT_ROWS], U8, name="x_scales", align_bytes=64)
            nc.vector.quantize_mx(
                out=x_words[u][:].bitcast(FP8X4),
                scales=x_scales[u][:],
                in_=x_grouped[u][:].rearrange("p c t -> p (c t)"),
            )

        def quantise_context(u):
            b, h = divmod(u, UNITS_PER_BATCH)
            if h == 0:
                c_words[b] = work.tile([P, C_ROWS], U32, name="c_words", align_bytes=64)
                c_scales[b] = work.tile([P, C_ROWS], U8, name="c_scales", align_bytes=64)
            piece = slice(h * PIECE_ROWS, (h + 1) * PIECE_ROWS)
            nc.vector.quantize_mx(
                out=c_words[b][:, piece].bitcast(FP8X4),
                scales=c_scales[b][:, piece],
                in_=c_grouped[u][:].rearrange("p j t -> p (j t)"),
            )

        def mid_pass(out, t, u, first_row, last_row):
            rows = slice(first_row, last_row)
            nc.tensor.matmul_mx(
                out=out,
                lhsT=w_words[:, t * P : (t + 1) * P].bitcast(FP8X4),
                lhsT_scale=w_scales[:, t * P : (t + 1) * P],
                rhs=x_words[u][:, rows].bitcast(FP8X4),
                rhs_scale=x_scales[u][:, rows],
                start=True,
                stop=True,
            )

        def mid_matmuls(u, planes):
            for t in planes:
                sums = q_banks.tile([P, PLANE_ROWS], F32, name="q_sums")
                q_sums[u, t] = sums
                mid_pass(sums[:, 0:256], t, u, 0, 256)
                mid_pass(sums[:, 256:PLANE_ROWS], t, u, 256, PLANE_ROWS)

        def mid_matmuls_joint(u):
            sums = q_banks.tile([P, PACK, P], F32, name="joint_sums", tag="q_sums")
            joint_sums[u] = sums
            for t in range(PACK):
                mid_pass(sums[:, t, :], t, u, PLANE_ROWS, UNIT_ROWS)

        def mid_bias(u, t, on_vector=False):
            if t == 0:
                q_planes[u] = work.tile([P, PACK, PLANE_ROWS], BF16, name="q_planes")
            bias = bias_cols[:, t : t + 1]
            if on_vector:
                nc.vector.tensor_scalar_add(out=q_planes[u][:, t, :], in0=q_sums[u, t][:], scalar1=bias)
            else:
                nc.scalar.activation(
                    out=q_planes[u][:, t, :], in_=q_sums[u, t][:], func=ACT.Identity, bias=bias, scale=1.0
                )

        def mid_bias_joint(u):
            nc.vector.tensor_tensor(
                out=grouped_tile(u)[:, PLANE_ROWS:, :],
                in0=joint_sums[u][:].rearrange("p t c -> p c t"),
                in1=bias_cols[:].unsqueeze(1).to_broadcast([P, P, PACK]),
                op=ALU.add,
            )

        def grouped_tile(u):
            if u not in q_grouped:
                q_grouped[u] = work.tile([P, UNIT_ROWS, PACK], BF16, name="q_grouped", align_bytes=64)
            return q_grouped[u]

        def mid_regroup_vector(u):
            nc.vector.tensor_copy(
                out=grouped_tile(u)[:, 0:PLANE_ROWS, :].rearrange("p (c i) t -> p c t i", i=4),
                in_=q_planes[u][:].rearrange("p t (c i) -> p c t i", i=4),
            )

        def mid_regroup_gpsimd(u):
            nc.gpsimd.tensor_scalar(
                out=grouped_tile(u)[:, 0:PLANE_ROWS, :],
                in0=q_planes[u][:].rearrange("p t c -> p c t"),
                scalar1=1.0,
                scalar2=0.0,
                op0=ALU.mult,
                op1=ALU.add,
            )

        def mid_quantise(u):
            q_words[u] = work.tile([P, UNIT_ROWS], U32, name="q_words", align_bytes=64)
            q_scales[u] = work.tile([P, UNIT_ROWS], U8, name="q_scales", align_bytes=64)
            nc.vector.quantize_mx(
                out=q_words[u][:].bitcast(FP8X4),
                scales=q_scales[u][:],
                in_=q_grouped[u][:].rearrange("p c t -> p (c t)"),
            )

        def back_matmuls(u, row_tiles):
            b = u // UNITS_PER_BATCH
            for r in row_tiles:
                sums = score_banks.tile([P, C_ROWS], F32, name="score_sums")
                score_sums[u, r] = sums
                nc.tensor.matmul_mx(
                    out=sums[:],
                    lhsT=q_words[u][:, r * P : (r + 1) * P].bitcast(FP8X4),
                    lhsT_scale=q_scales[u][:, r * P : (r + 1) * P],
                    rhs=c_words[b][:].bitcast(FP8X4),
                    rhs_scale=c_scales[b][:],
                    start=True,
                    stop=True,
                )

        def start_back(u):
            probs[u] = result.tile([P, ROW_TILES, C_ROWS], F32, name="probs")
            neg_max[u] = result.tile([P, ROW_TILES], F32, name="neg_max")

        def add_mask(u, r):
            nc.vector.scalar_tensor_tensor(
                out=probs[u][:, r, :],
                in0=cbit_minus_1[:, u // UNITS_PER_BATCH, :],
                scalar=mask_weight[:, r, u : u + 1],
                in1=score_sums[u, r][:],
                op0=ALU.mult,
                op1=ALU.add,
            )

        def row_maximum(u, r):
            nc.vector.tensor_reduce(
                out=neg_max[u][:, r : r + 1], in_=probs[u][:, r, :], axis=AXIS.X, op=ALU.max, negate=True
            )

        def back_mask_and_maximum(u, r):
            if r == 0:
                start_back(u)
            add_mask(u, r)
            add_mask(u, r + 1)
            row_maximum(u, r)
            row_maximum(u, r + 1)

        def back_exp(u, tiles=range(ROW_TILES)):
            for r in tiles:
                if r == 0:
                    row_sum[u] = result.tile([P, ROW_TILES], F32, name="row_sum")
                nc.scalar.activation(
                    out=probs[u][:, r, :],
                    in_=probs[u][:, r, :],
                    func=ACT.Exp,
                    bias=neg_max[u][:, r : r + 1],
                    scale=1.0,
                    accum_out=row_sum[u][:, r : r + 1],
                )

        def back_reciprocal(u, first=0, last=ROW_TILES):
            if first == 0:
                inv_sum[u] = result.tile([P, ROW_TILES], F32, name="inv_sum")
            nc.vector.reciprocal(out=inv_sum[u][:, first:last], in_=row_sum[u][:, first:last])

        def divide(engine, u, r):
            probabilities = probs[u][:, r, :]
            factor = inv_sum[u][:, r : r + 1]
            engine.tensor_scalar(
                out=probabilities, in0=probabilities, scalar1=factor, scalar2=0.0, op0=ALU.mult, op1=ALU.add
            )

        def divide_on_scalar(u, r):
            probabilities = probs[u][:, r, :]
            nc.scalar.activation(
                out=probabilities, in_=probabilities, func=ACT.Copy, scale=inv_sum[u][:, r : r + 1]
            )

        def store(u, r):
            b, h = divmod(u, UNITS_PER_BATCH)
            rows = out[b, h * UNIT_ROWS : (h + 1) * UNIT_ROWS, :].rearrange("(p r) j -> p r j", r=ROW_TILES)
            nc.sync.dma_start(out=rows[:, r, :], in_=probs[u][:, r, :])

        def back_divide_and_store(u, on_gpsimd):
            for r in range(on_gpsimd):
                divide(nc.gpsimd, u, r)
                store(u, r)

        def back_divide_and_store_rest(u, on_gpsimd):
            for r in range(on_gpsimd, ROW_TILES):
                divide_on_scalar(u, r)
                store(u, r)

        def keep_warm(passes):
            idle = score_banks.tile([P, C_ROWS], F32, name="idle", tag="score_sums")
            for i in range(passes):
                nc.tensor.matmul(out=idle[:], lhsT=cbit_rows[:, 0:P], rhs=cbit_rows[:], start=True, stop=True)

        def exists(u):
            return 0 <= u < UNITS

        keep_warm(5)
        prepare_context_bits()
        order_weight_codes()
        turn_query_rows(0, 0)
        copy_query_rows(0, 0)
        turn_query_rows(0, 1)
        copy_query_rows(0, 1, on_vector=True)
        spread_context_bits(0)
        copy_context_bits(0)
        prepare_bias()
        spread_context_bits(2)
        quantise_query(0)
        order_weight_scales()
        mid_matmuls(0, range(0, Q_BANKS))
        mid_bias(0, 0)
        mid_bias(0, 1)
        copy_context_bits(2)
        mid_bias(0, 2, on_vector=True)
        prepare_mask_weight()
        mid_matmuls(0, range(Q_BANKS, PACK))
        mid_matmuls_joint(0)
        mid_bias(0, 3, on_vector=True)
        mid_bias_joint(0)
        mid_regroup_vector(0)
        spread_context_bits(4)
        turn_context_rows(0)
        turn_context_rows(1)
        copy_context_bits(4)
        copy_context_rows(0)
        copy_context_rows(1)
        turn_query_rows(1, 0)
        turn_query_rows(1, 1)
        copy_query_rows(1, 0)
        copy_query_rows(1, 1)
        spread_context_bits(6, q_banks, "q_sums")
        turn_query_rows(2, 0)
        copy_query_rows(2, 0)
        copy_context_bits(6)
        mid_quantise(0)
        quantise_context(0)
        quantise_context(1)
        back_matmuls(0, range(0, SCORE_BANKS))
        quantise_query(1)
        mid_matmuls(1, range(0, Q_BANKS))
        back_mask_and_maximum(0, 0)
        back_matmuls(0, range(SCORE_BANKS, ROW_TILES))
        mid_bias(1, 0)
        mid_matmuls(1, range(Q_BANKS, PACK))
        mid_matmuls_joint(1)
        mid_bias(1, 1)
        mid_bias(1, 2)
        mid_bias(1, 3)
        turn_query_rows(2, 1)
        turn_context_rows(2)
        copy_query_rows(2, 1)
        copy_context_rows(2)
        back_mask_and_maximum(0, 2)
        front_transposes(3)
        front_copies(3)
        quantise_query(2)
        mid_matmuls(2, range(0, Q_BANKS))
        mid_bias_joint(1)
        mid_regroup_gpsimd(1)
        mid_quantise(1)
        back_matmuls(1, range(0, SCORE_BANKS))
        mid_bias(2, 0)
        mid_bias(2, 1)
        mid_bias(2, 2)
        quantise_context(2)
        quantise_query(3)
        quantise_context(3)
        back_mask_and_maximum(1, 0)
        back_matmuls(1, range(SCORE_BANKS, ROW_TILES))
        back_exp(0)
        mid_matmuls(2, range(Q_BANKS, PACK))
        mid_matmuls_joint(2)
        mid_bias(2, 3)
        front_transposes(4)
        front_copies(4)
        back_mask_and_maximum(1, 2)
        mid_bias_joint(2)
        mid_regroup_gpsimd(2)
        mid_matmuls(3, range(0, Q_BANKS))
        mid_bias(3, 0)
        mid_matmuls(3, range(Q_BANKS, PACK))
        mid_matmuls_joint(3)
        mid_bias(3, 1)
        mid_bias(3, 2)
        mid_bias(3, 3)
        mid_quantise(2)
        back_matmuls(2, range(0, SCORE_BANKS))
        front_transposes(5)
        quantise_context(4)
        quantise_query(4)
        back_reciprocal(0)
        mid_bias_joint(3)
        for step in range(2, last - 1):
            back_divide_and_store(step - 2, GPSIMD_TILES)
            mid_regroup_gpsimd(step + 1)
            mid_matmuls(step + 2, range(0, Q_BANKS))
            back_matmuls(step, range(SCORE_BANKS, ROW_TILES))
            mid_matmuls(step + 2, range(Q_BANKS, PACK))
            mid_matmuls_joint(step + 2)
            if exists(step + 4):
                front_transposes(step + 4)
            back_mask_and_maximum(step, 0)
            back_mask_and_maximum(step, 2)
            if exists(step + 3):
                front_copies(step + 3)
            for t in range(PACK):
                mid_bias(step + 2, t)
            back_exp(step - 1)
            back_divide_and_store_rest(step - 2, GPSIMD_TILES)
            mid_quantise(step + 1)
            back_matmuls(step + 1, range(0, SCORE_BANKS))
            if exists(step + 3):
                quantise_context(step + 3)
                quantise_query(step + 3)
            back_reciprocal(step - 1)
            mid_bias_joint(step + 2)
        back_divide_and_store(last - 3, 2)
        mid_regroup_gpsimd(last)
        back_matmuls(last - 1, range(SCORE_BANKS, ROW_TILES))
        back_exp(last - 2)
        back_divide_and_store_rest(last - 3, 2)
        back_mask_and_maximum(last - 1, 0)
        add_mask(last - 1, 2)
        add_mask(last - 1, 3)
        mid_quantise(last)
        back_matmuls(last, range(0, SCORE_BANKS))
        row_maximum(last - 1, 2)
        row_maximum(last - 1, 3)
        back_exp(last - 1)
        back_reciprocal(last - 2)
        back_divide_and_store(last - 2, 2)
        back_divide_and_store_rest(last - 2, 2)
        start_back(last)
        add_mask(last, 0)
        add_mask(last, 1)
        back_matmuls(last, range(SCORE_BANKS, ROW_TILES))
        back_reciprocal(last - 1)
        row_maximum(last, 0)
        row_maximum(last, 1)
        back_exp(last, [0, 1])
        back_divide_and_store(last - 1, 2)
        divide_on_scalar(last - 1, 2)
        store(last - 1, 2)
        back_mask_and_maximum(last, 2)
        divide(nc.vector, last - 1, 3)
        store(last - 1, 3)
        back_exp(last, [2, 3])
        back_reciprocal(last, 0, 3)
        for r in range(ROW_TILES):
            if r == 2:
                back_reciprocal(last, 3, 4)
            divide(nc.vector, last, r)
            store(last, r)
